import numpy as np
import ml_dtypes


def mxq(x, axis, fmt="e4m3"):
    dtype, down = {"e4m3": (ml_dtypes.float8_e4m3fn, 7), "e5m2": (ml_dtypes.float8_e5m2, 14)}[fmt]
    v = np.moveaxis(np.asarray(x, np.float32).astype(ml_dtypes.bfloat16).astype(np.float64), axis, -1)
    blocks = v.reshape(v.shape[:-1] + (-1, 32))
    amax = np.abs(blocks).max(-1, keepdims=True)
    byte = np.maximum(np.where(amax > 0, np.frexp(amax)[1] - 1 + 127, 0) - down, 1)
    scale = np.exp2(byte - 127.0)
    codes = (blocks / scale).astype(np.float32).astype(dtype).astype(np.float64)
    return np.moveaxis((codes * scale).reshape(v.shape), -1, axis)


WIDE = False


def mx_kscale(k):
    if not WIDE:
        return np.ones(k)
    levels = np.array([10, -10, 5, -5, 0])
    a = np.random.permutation(np.resize(levels, k // 512 * 4)).reshape(k // 512, 4)
    idx = np.arange(k)
    return np.exp2(a[idx // 512, idx % 128 // 32])


BF16 = ml_dtypes.bfloat16


def bf(x):
    return np.asarray(x, np.float32).astype(BF16)


def f64(x):
    return np.asarray(x).astype(np.float64)


N, RANK, H, W, B = 4, 512, 16, 32, 4096
S = H * W
EPS = 1e-5
XS = 0.01


def setup_inputs():
    t = mx_kscale(RANK)
    U = np.random.standard_normal((N, S, RANK)) * 0.5 / np.sqrt(S)
    U[0] = U[0] * t
    return {"x": bf((np.random.standard_normal((B, 1, H, W)) + 0.5) * XS),
            "U": bf(U),
            "C": bf(np.random.standard_normal((S, RANK)) / np.sqrt(RANK) / t),
            "beta": bf(np.random.standard_normal(S) * 0.5),
            "gamma": bf(1.25 + 0.1 * np.random.standard_normal(1)),
            "bn_bias": bf(0.3 + 0.05 * np.random.standard_normal(1))}


def reference(x, U, C, beta, gamma, bn_bias):
    x = f64(x)
    b = x.shape[0]
    mean = x.mean(axis=(0, 2, 3), keepdims=True)
    var = x.var(axis=(0, 2, 3), keepdims=True)
    xn = (x - mean) * (1.0 / np.sqrt(var + EPS))
    xn = xn * f64(gamma).reshape(1, -1, 1, 1) + f64(bn_bias).reshape(1, -1, 1, 1)
    z = xn.reshape(b, S)
    t = mxq(z, 1, "e4m3") @ mxq(f64(U), 1, "e4m3")
    h = t[0]
    for n in range(1, N):
        h = t[n] * h + h
    out = (mxq(h, 1, "e4m3") @ mxq(f64(C), 1, "e4m3").T) + f64(beta)
    return out.reshape(b, 1, H, W)

@@ -1,0 +1,322 @@
+import concourse.bass as bass
+import concourse.mybir as mybir
+import concourse.tile as tile
+from concourse.masks import make_identity
+
+F32 = mybir.dt.float32
+BF16 = mybir.dt.bfloat16
+U32 = mybir.dt.uint32
+U8 = mybir.dt.uint8
+FP8X4 = mybir.dt.float8_e4m3fn_x4
+ACT = mybir.ActivationFunctionType
+ALU = mybir.AluOpType
+
+P = 128
+BATCH = 4096
+PIXELS = 512
+RANK = 512
+DEGREE = 4
+EPS = 1e-5
+BLOCKS = BATCH // P
+GROUP = 4
+GROUPS = BLOCKS // GROUP
+CHUNKS = RANK // P
+HALF = GROUP // 2
+COUNT = BATCH * PIXELS
+VECTOR_COUNT = GROUPS * HALF * PIXELS
+
+FLOPS = 2 * BATCH * PIXELS * RANK * (DEGREE + 1)
+
+
+def tile_generator_pa_t_kernel(tc, x, U, C, beta, gamma, bn_bias, out):
+    nc = tc.nc
+    x_rows = x.rearrange("(p j) o h w -> p j (o h w)", j=BLOCKS)
+    out_rows = out.rearrange("(p j) o h w -> p j (o h w)", j=BLOCKS)
+
+    with tc.tile_pool(name="const", bufs=1) as const, tc.tile_pool(
+        name="keep", bufs=1
+    ) as keep, tc.tile_pool(name="small", bufs=1) as small, tc.tile_pool(
+        name="stage", bufs=2
+    ) as stage, tc.tile_pool(name="work", bufs=3) as work, tc.psum_pool(
+        name="psum", bufs=1
+    ) as psum:
+        one_t = const.tile([P, 1], F32)
+        nc.vector.memset(one_t[:], 1.0)
+        warm = const.tile([P, 1], F32)
+        nc.scalar.activation(out=warm[:], in_=one_t[:], func=ACT.Sqrt)
+        ident_f32 = const.tile([P, P], F32)
+        make_identity(nc, ident_f32[:])
+        ident_bf = const.tile([P, P], BF16)
+        make_identity(nc, ident_bf[:])
+        share_bf = const.tile([P, P], BF16)
+        nc.vector.memset(share_bf[:], 1.0 / P)
+        inv_count = const.tile([P, P], F32)
+        nc.vector.memset(inv_count[:], 1.0 / COUNT)
+        gamma_b = const.tile([P, 1], BF16)
+        nc.scalar.dma_start(out=gamma_b[:], in_=gamma.partition_broadcast(P))
+        bias_b = const.tile([P, 1], BF16)
+        nc.scalar.dma_start(out=bias_b[:], in_=bn_bias.partition_broadcast(P))
+
+        x_sb = []
+        for g in range(GROUPS):
+            x_g = keep.tile([P, GROUP, PIXELS], BF16, name="x%d" % g)
+            nc.sync.dma_start(out=x_g[:], in_=x_rows[:, g * GROUP : (g + 1) * GROUP, :])
+            x_sb.append(x_g)
+        u_raw = []
+        for n in range(DEGREE):
+            u_n = keep.tile([P, 4, RANK], BF16, name="u_raw%d" % n)
+            nc.sync.dma_start(
+                out=u_n[:].rearrange("w (u e) c -> w u (e c)", u=2),
+                in_=U[n].rearrange("(u w e) c -> w u (e c)", u=2, e=2),
+            )
+            u_raw.append(u_n)
+        c_raw = keep.tile([P, CHUNKS, RANK], BF16)
+        nc.sync.dma_start(out=c_raw[:], in_=C.rearrange("(q p) r -> p q r", p=P))
+        beta_bc = const.tile([P, PIXELS], BF16)
+        nc.sync.dma_start(out=beta_bc[:], in_=beta.partition_broadcast(P))
+
+        xt_words = keep.tile([P, GROUPS, GROUP * P, 2], F32, align_bytes=64)
+        stats = small.tile([P, GROUPS * HALF, 6], F32)
+        squares = small.tile([P, GROUPS], F32)
+        column_sums = psum.tile([P, PIXELS], F32, tag="o", bufs=2)
+        for g in range(GROUPS):
+            for jj in range(HALF):
+                nc.vector.bn_stats(out=stats[:, g * HALF + jj, :], in_=x_sb[g][:, jj, :])
+            unread = stage.tile([P, GROUP - HALF, PIXELS], BF16, tag="unread")
+            nc.scalar.activation(
+                out=unread[:],
+                in_=x_sb[g][:, HALF:GROUP, :],
+                func=ACT.Square,
+                accum_out=squares[:, g : g + 1],
+            )
+            for jj in range(HALF, GROUP):
+                nc.tensor.matmul(
+                    out=column_sums[:],
+                    lhsT=share_bf[:],
+                    rhs=x_sb[g][:, jj, :],
+                    start=(g == 0 and jj == HALF),
+                    stop=(g == GROUPS - 1 and jj == GROUP - 1),
+                )
+        for g in range(GROUPS):
+            for pair in range(GROUP // 2):
+                xt = psum.tile([P, 2, 2 * P], F32, tag="bank", bufs=6)
+                for jj in range(2):
+                    words = x_sb[g][:, 2 * pair + jj, :].bitcast(F32)
+                    for u in range(2):
+                        nc.tensor.transpose(
+                            xt[:, u, jj * P : (jj + 1) * P], words[:, u * P : (u + 1) * P], ident_f32[:]
+                        )
+                nc.scalar.copy(
+                    out=xt_words[:, g, 2 * pair * P : 2 * (pair + 1) * P, :],
+                    in_=xt[:].rearrange("w u c -> w c u"),
+                )
+        mean_var = small.tile([P, 2], F32)
+        nc.vector.bn_aggr(out=mean_var[:], in_=stats[:].rearrange("p s d -> p (s d)"))
+        sum_share = small.tile([P, 1], F32)
+        nc.vector.tensor_reduce(
+            out=sum_share[:], in_=column_sums[:], axis=mybir.AxisListType.X, op=ALU.add
+        )
+        square_sum = small.tile([P, 1], F32)
+        nc.vector.tensor_reduce(
+            out=square_sum[:], in_=squares[:], axis=mybir.AxisListType.X, op=ALU.add
+        )
+        second = small.tile([P, 1], F32)
+        nc.vector.scalar_tensor_tensor(
+            out=second[:], in0=mean_var[:, 0:1], scalar=mean_var[:, 0:1], in1=mean_var[:, 1:2],
+            op0=ALU.mult, op1=ALU.add,
+        )
+        sums = small.tile([P, 2], F32)
+        nc.vector.scalar_tensor_tensor(
+            out=sums[:, 0:1], in0=mean_var[:, 0:1], scalar=float(VECTOR_COUNT), in1=sum_share[:],
+            op0=ALU.mult, op1=ALU.add,
+        )
+        nc.vector.scalar_tensor_tensor(
+            out=sums[:, 1:2], in0=second[:], scalar=float(VECTOR_COUNT), in1=square_sum[:],
+            op0=ALU.mult, op1=ALU.add,
+        )
+        moments_ps = psum.tile([P, 2], F32, tag="o", bufs=2)
+        nc.tensor.matmul(out=moments_ps[:], lhsT=inv_count[:], rhs=sums[:], start=True, stop=True)
+        moments = small.tile([P, 2], F32)
+        nc.vector.tensor_copy(out=moments[:], in_=moments_ps[:])
+        minus_var = small.tile([P, 1], F32)
+        nc.vector.scalar_tensor_tensor(
+            out=minus_var[:], in0=moments[:, 0:1], scalar=moments[:, 0:1], in1=moments[:, 1:2],
+            op0=ALU.mult, op1=ALU.subtract,
+        )
+        var_eps = small.tile([P, 1], F32)
+        nc.vector.tensor_scalar(
+            out=var_eps[:], in0=minus_var[:], scalar1=-1.0, scalar2=EPS, op0=ALU.mult, op1=ALU.add
+        )
+        std = small.tile([P, 1], F32)
+        nc.scalar.activation(out=std[:], in_=var_eps[:], func=ACT.Sqrt)
+        rstd = small.tile([P, 1], F32)
+        nc.vector.reciprocal(out=rstd[:], in_=std[:])
+        gain = small.tile([P, 1], F32)
+        nc.vector.tensor_tensor(out=gain[:], in0=rstd[:], in1=gamma_b[:], op=ALU.mult)
+        minus_gain = small.tile([P, 1], F32)
+        nc.vector.scalar_tensor_tensor(
+            out=minus_gain[:], in0=rstd[:], scalar=-1.0, in1=gamma_b[:], op0=ALU.mult, op1=ALU.mult
+        )
+        shift = small.tile([P, 1], F32)
+        nc.vector.scalar_tensor_tensor(
+            out=shift[:], in0=moments[:, 0:1], scalar=minus_gain[:], in1=bias_b[:],
+            op0=ALU.mult, op1=ALU.add,
+        )
+
+        u_codes = keep.tile([P, DEGREE, RANK], U32, align_bytes=64)
+        u_scales = keep.tile([P, DEGREE, RANK], U8, align_bytes=64)
+        for n in range(DEGREE):
+            u_grp = stage.tile([P, RANK, 4], BF16, tag="u_grp", align_bytes=64)
+            dst = u_grp[:].rearrange("p (c i) t -> p c t i", i=4)
+            src = u_raw[n][:].rearrange("p t (c i) -> p c t i", i=4)
+            if n % 2 == 0:
+                nc.scalar.copy(out=dst, in_=src)
+            else:
+                nc.gpsimd.tensor_scalar(
+                    out=dst, in0=src, scalar1=1.0, scalar2=0.0, op0=ALU.mult, op1=ALU.add
+                )
+            nc.vector.quantize_mx(
+                out=u_codes[:, n, :].bitcast(FP8X4),
+                scales=u_scales[:, n, :],
+                in_=u_grp[:].rearrange("p c t -> p (c t)"),
+            )
+
+        z_codes = keep.tile([P, GROUPS, GROUP * P], U32, align_bytes=64)
+        z_scales = keep.tile([P, GROUPS, GROUP * P], U8, align_bytes=64)
+
+        def prepare_z(g):
+            z_grp = stage.tile([P, GROUP * P * 4], BF16, tag="z_grp", align_bytes=64)
+            nc.vector.tensor_scalar(
+                out=z_grp[:],
+                in0=xt_words[:, g, :, :].rearrange("w c u -> w (c u)").bitcast(BF16),
+                scalar1=gain[:],
+                scalar2=shift[:],
+                op0=ALU.mult,
+                op1=ALU.add,
+            )
+            nc.vector.quantize_mx(
+                out=z_codes[:, g, :].bitcast(FP8X4), scales=z_scales[:, g, :], in_=z_grp[:]
+            )
+
+        c_codes = keep.tile([P, PIXELS], U32, align_bytes=64)
+        c_scales = keep.tile([P, PIXELS], U8, align_bytes=64)
+
+        def prepare_c():
+            c_grp = keep.tile([P, PIXELS, CHUNKS], BF16, align_bytes=64)
+            for half in range(2):
+                ct = psum.tile([P, CHUNKS, 2 * P], BF16, tag="o", bufs=2)
+                for qq in range(2):
+                    for r in range(CHUNKS):
+                        nc.tensor.transpose(
+                            ct[:, r, qq * P : (qq + 1) * P],
+                            c_raw[:, 2 * half + qq, r * P : (r + 1) * P],
+                            ident_bf[:],
+                        )
+                nc.scalar.copy(
+                    out=c_grp[:, 2 * half * P : 2 * (half + 1) * P, :],
+                    in_=ct[:].rearrange("p r x -> p x r"),
+                )
+            nc.vector.quantize_mx(
+                out=c_codes[:].bitcast(FP8X4),
+                scales=c_scales[:],
+                in_=c_grp[:].rearrange("p x r -> p (x r)"),
+            )
+
+        h_values = {}
+        h_words = {}
+        o_banks = {}
+
+        def stage_one(j):
+            g = j // GROUP
+            cols = slice((j % GROUP) * P, (j % GROUP + 1) * P)
+            t = []
+            for n in range(DEGREE):
+                t_n = psum.tile([P, CHUNKS, P], F32, tag="bank", bufs=6, name="t%d" % n)
+                for r in range(CHUNKS):
+                    ranks = slice(r * P, (r + 1) * P)
+                    nc.tensor.matmul_mx(
+                        out=t_n[:, r, :],
+                        lhsT=u_codes[:, n, ranks].bitcast(FP8X4),
+                        lhsT_scale=u_scales[:, n, ranks],
+                        rhs=z_codes[:, g, cols].bitcast(FP8X4),
+                        rhs_scale=z_scales[:, g, cols],
+                        start=True,
+                        stop=True,
+                    )
+                t.append(t_n[:].rearrange("p r b -> p b r"))
+            t0_sb = work.tile([P, P, CHUNKS], F32, tag="t0_sb")
+            nc.scalar.copy(out=t0_sb[:], in_=t[0])
+            t2_sb = work.tile([P, P, CHUNKS], F32, tag="t2_sb")
+            nc.scalar.activation(out=t2_sb[:], in_=t[2], func=ACT.Copy, bias=1.0)
+            left = work.tile([P, P, CHUNKS], F32, tag="left")
+            nc.vector.scalar_tensor_tensor(
+                out=left[:], in0=t[1], scalar=1.0, in1=t0_sb[:], op0=ALU.add, op1=ALU.mult
+            )
+            right = work.tile([P, P, CHUNKS], F32, tag="right")
+            nc.vector.scalar_tensor_tensor(
+                out=right[:], in0=t[3], scalar=1.0, in1=t2_sb[:], op0=ALU.add, op1=ALU.mult
+            )
+            h_grp = work.tile([P, P, CHUNKS], BF16, tag="h_grp", align_bytes=64)
+            nc.gpsimd.tensor_tensor(out=h_grp[:], in0=left[:], in1=right[:], op=ALU.mult)
+            h_values[j] = h_grp
+
+        def quantise_h(j):
+            h_grp = h_values[j]
+            h_codes = work.tile([P, P], U32, tag="h_codes", align_bytes=64)
+            h_scales = work.tile([P, P], U8, tag="h_scales", align_bytes=64)
+            nc.vector.quantize_mx(
+                out=h_codes[:].bitcast(FP8X4),
+                scales=h_scales[:],
+                in_=h_grp[:].rearrange("p b r -> p (b r)"),
+            )
+            h_words[j] = (h_codes, h_scales)
+
+        out_tiles = {}
+
+        def stage_two(j):
+            h_codes, h_scales = h_words[j]
+            o = psum.tile([P, PIXELS], F32, tag="o", bufs=2)
+            nc.tensor.matmul_mx(
+                out=o[:],
+                lhsT=h_codes[:].bitcast(FP8X4),
+                lhsT_scale=h_scales[:],
+                rhs=c_codes[:].bitcast(FP8X4),
+                rhs_scale=c_scales[:],
+                start=True,
+                stop=True,
+            )
+            o_banks[j] = o
+
+        def add_beta(j):
+            g = j // GROUP
+            if j % GROUP == 0:
+                out_tiles[g] = work.tile([P, GROUP, PIXELS], F32, tag="out_sb", name="out_sb")
+            out_sb = out_tiles[g]
+            o = o_banks[j]
+            if j % 2 == 0:
+                nc.vector.tensor_tensor(
+                    out=out_sb[:, j % GROUP, :], in0=o[:], in1=beta_bc[:], op=ALU.add
+                )
+            else:
+                o_sb = work.tile([P, PIXELS], F32, tag="o_sb")
+                nc.scalar.copy(out=o_sb[:], in_=o[:])
+                nc.gpsimd.tensor_tensor(
+                    out=out_sb[:, j % GROUP, :], in0=o_sb[:], in1=beta_bc[:], op=ALU.add
+                )
+            if j % GROUP == GROUP - 1:
+                nc.sync.dma_start(
+                    out=out_rows[:, g * GROUP : (g + 1) * GROUP, :], in_=out_sb[:]
+                )
+
+        prepare_z(0)
+        prepare_c()
+        for step in range(BLOCKS + 2):
+            if step < BLOCKS:
+                if step % GROUP == 0 and step // GROUP + 1 < GROUPS:
+                    prepare_z(step // GROUP + 1)
+                stage_one(step)
+            if 0 <= step - 1 < BLOCKS:
+                quantise_h(step - 1)
+                stage_two(step - 1)
+            if 0 <= step - 2:
+                add_beta(step - 2)

@@ -25,6 +25,10 @@ HALF = GROUP // 2
 COUNT = BATCH * PIXELS
 VECTOR_COUNT = GROUPS * HALF * PIXELS
 
+QUANTISE_LAG = GROUP + 1
+MATMUL_LAG = QUANTISE_LAG + 1
+ADD_LAG = MATMUL_LAG + 1
+
 FLOPS = 2 * BATCH * PIXELS * RANK * (DEGREE + 1)
 
 
@@ -256,30 +260,33 @@ def tile_generator_pa_t_kernel(tc, x, U, C, beta, gamma, bn_bias, out):
             nc.vector.scalar_tensor_tensor(
                 out=right[:], in0=t[3], scalar=1.0, in1=t2_sb[:], op0=ALU.add, op1=ALU.mult
             )
-            h_grp = work.tile([P, P, CHUNKS], BF16, tag="h_grp", align_bytes=64)
-            nc.gpsimd.tensor_tensor(out=h_grp[:], in0=left[:], in1=right[:], op=ALU.mult)
-            h_values[j] = h_grp
+            if j % GROUP == 0:
+                h_values[g] = work.tile(
+                    [P, GROUP * P, CHUNKS], BF16, tag="h_grp", name="h_grp", align_bytes=64
+                )
+            nc.gpsimd.tensor_tensor(out=h_values[g][:, cols, :], in0=left[:], in1=right[:], op=ALU.mult)
 
-        def quantise_h(j):
-            h_grp = h_values[j]
-            h_codes = work.tile([P, P], U32, tag="h_codes", align_bytes=64)
-            h_scales = work.tile([P, P], U8, tag="h_scales", align_bytes=64)
+        def quantise_h(g):
+            h_grp = h_values[g]
+            h_codes = work.tile([P, GROUP * P], U32, tag="h_codes", align_bytes=64)
+            h_scales = work.tile([P, GROUP * P], U8, tag="h_scales", align_bytes=64)
             nc.vector.quantize_mx(
                 out=h_codes[:].bitcast(FP8X4),
                 scales=h_scales[:],
                 in_=h_grp[:].rearrange("p b r -> p (b r)"),
             )
-            h_words[j] = (h_codes, h_scales)
+            h_words[g] = (h_codes, h_scales)
 
         out_tiles = {}
 
         def stage_two(j):
-            h_codes, h_scales = h_words[j]
+            h_codes, h_scales = h_words[j // GROUP]
+            cols = slice((j % GROUP) * P, (j % GROUP + 1) * P)
             o = psum.tile([P, PIXELS], F32, tag="o", bufs=2)
             nc.tensor.matmul_mx(
                 out=o[:],
-                lhsT=h_codes[:].bitcast(FP8X4),
-                lhsT_scale=h_scales[:],
+                lhsT=h_codes[:, cols].bitcast(FP8X4),
+                lhsT_scale=h_scales[:, cols],
                 rhs=c_codes[:].bitcast(FP8X4),
                 rhs_scale=c_scales[:],
                 start=True,
@@ -293,7 +300,7 @@ def tile_generator_pa_t_kernel(tc, x, U, C, beta, gamma, bn_bias, out):
                 out_tiles[g] = work.tile([P, GROUP, PIXELS], F32, tag="out_sb", name="out_sb")
             out_sb = out_tiles[g]
             o = o_banks[j]
-            if j % 2 == 0:
+            if j % GROUP < GROUP - 1:
                 nc.vector.tensor_tensor(
                     out=out_sb[:, j % GROUP, :], in0=o[:], in1=beta_bc[:], op=ALU.add
                 )
@@ -309,14 +316,17 @@ def tile_generator_pa_t_kernel(tc, x, U, C, beta, gamma, bn_bias, out):
                 )
 
         prepare_z(0)
+        prepare_z(1)
         prepare_c()
-        for step in range(BLOCKS + 2):
+        for step in range(BLOCKS + ADD_LAG + 1):
             if step < BLOCKS:
-                if step % GROUP == 0 and step // GROUP + 1 < GROUPS:
-                    prepare_z(step // GROUP + 1)
                 stage_one(step)
-            if 0 <= step - 1 < BLOCKS:
-                quantise_h(step - 1)
-                stage_two(step - 1)
-            if 0 <= step - 2:
-                add_beta(step - 2)
+            g = (step - QUANTISE_LAG) // GROUP
+            if (step - QUANTISE_LAG) % GROUP == 0 and 0 <= g < GROUPS:
+                quantise_h(g)
+                if g + 2 < GROUPS:
+                    prepare_z(g + 2)
+            if 0 <= step - MATMUL_LAG < BLOCKS:
+                stage_two(step - MATMUL_LAG)
+            if 0 <= step - ADD_LAG < BLOCKS:
+                add_beta(step - ADD_LAG)

@@ -79,7 +79,6 @@ def tile_generator_pa_t_kernel(tc, x, U, C, beta, gamma, bn_bias, out):
         beta_bc = const.tile([P, PIXELS], BF16)
         nc.sync.dma_start(out=beta_bc[:], in_=beta.partition_broadcast(P))
 
-        xt_words = keep.tile([P, GROUPS, GROUP * P, 2], F32, align_bytes=64)
         stats = small.tile([P, GROUPS * HALF, 6], F32)
         squares = small.tile([P, GROUPS], F32)
         column_sums = psum.tile([P, PIXELS], F32, tag="o", bufs=2)
@@ -100,19 +99,6 @@ def tile_generator_pa_t_kernel(tc, x, U, C, beta, gamma, bn_bias, out):
                     rhs=x_sb[g][:, jj, :],
                     start=(g == 0 and jj == HALF),
                     stop=(g == GROUPS - 1 and jj == GROUP - 1),
-                )
-        for g in range(GROUPS):
-            for pair in range(GROUP // 2):
-                xt = psum.tile([P, 2, 2 * P], F32, tag="bank", bufs=6)
-                for jj in range(2):
-                    words = x_sb[g][:, 2 * pair + jj, :].bitcast(F32)
-                    for u in range(2):
-                        nc.tensor.transpose(
-                            xt[:, u, jj * P : (jj + 1) * P], words[:, u * P : (u + 1) * P], ident_f32[:]
-                        )
-                nc.scalar.copy(
-                    out=xt_words[:, g, 2 * pair * P : 2 * (pair + 1) * P, :],
-                    in_=xt[:].rearrange("w u c -> w c u"),
                 )
         mean_var = small.tile([P, 2], F32)
         nc.vector.bn_aggr(out=mean_var[:], in_=stats[:].rearrange("p s d -> p (s d)"))
@@ -167,29 +153,28 @@ def tile_generator_pa_t_kernel(tc, x, U, C, beta, gamma, bn_bias, out):
             op0=ALU.mult, op1=ALU.add,
         )
 
-        u_codes = keep.tile([P, DEGREE, RANK], U32, align_bytes=64)
-        u_scales = keep.tile([P, DEGREE, RANK], U8, align_bytes=64)
-        for n in range(DEGREE):
-            u_grp = stage.tile([P, RANK, 4], BF16, tag="u_grp", align_bytes=64)
-            dst = u_grp[:].rearrange("p (c i) t -> p c t i", i=4)
-            src = u_raw[n][:].rearrange("p t (c i) -> p c t i", i=4)
-            if n % 2 == 0:
-                nc.scalar.copy(out=dst, in_=src)
-            else:
-                nc.gpsimd.tensor_scalar(
-                    out=dst, in0=src, scalar1=1.0, scalar2=0.0, op0=ALU.mult, op1=ALU.add
+        xt_words = keep.tile([P, GROUPS, GROUP * P, 2], F32, align_bytes=64)
+
+        def transpose_x(g):
+            for pair in range(GROUP // 2):
+                xt = psum.tile([P, 2, 2 * P], F32, tag="bank", bufs=6)
+                for jj in range(2):
+                    words = x_sb[g][:, 2 * pair + jj, :].bitcast(F32)
+                    for u in range(2):
+                        nc.tensor.transpose(
+                            xt[:, u, jj * P : (jj + 1) * P], words[:, u * P : (u + 1) * P], ident_f32[:]
+                        )
+                nc.scalar.copy(
+                    out=xt_words[:, g, 2 * pair * P : 2 * (pair + 1) * P, :],
+                    in_=xt[:].rearrange("w u c -> w c u"),
                 )
-            nc.vector.quantize_mx(
-                out=u_codes[:, n, :].bitcast(FP8X4),
-                scales=u_scales[:, n, :],
-                in_=u_grp[:].rearrange("p c t -> p (c t)"),
-            )
 
         z_codes = keep.tile([P, GROUPS, GROUP * P], U32, align_bytes=64)
         z_scales = keep.tile([P, GROUPS, GROUP * P], U8, align_bytes=64)
+        z_values = {}
 
-        def prepare_z(g):
-            z_grp = stage.tile([P, GROUP * P * 4], BF16, tag="z_grp", align_bytes=64)
+        def normalise(g):
+            z_grp = stage.tile([P, GROUP * P * 4], BF16, tag="z_grp", bufs=3, align_bytes=64)
             nc.vector.tensor_scalar(
                 out=z_grp[:],
                 in0=xt_words[:, g, :, :].rearrange("w c u -> w (c u)").bitcast(BF16),
@@ -198,8 +183,34 @@ def tile_generator_pa_t_kernel(tc, x, U, C, beta, gamma, bn_bias, out):
                 op0=ALU.mult,
                 op1=ALU.add,
             )
+            z_values[g] = z_grp
+
+        def quantise_z(g):
             nc.vector.quantize_mx(
-                out=z_codes[:, g, :].bitcast(FP8X4), scales=z_scales[:, g, :], in_=z_grp[:]
+                out=z_codes[:, g, :].bitcast(FP8X4), scales=z_scales[:, g, :], in_=z_values[g][:]
+            )
+
+        u_codes = keep.tile([P, DEGREE, RANK], U32, align_bytes=64)
+        u_scales = keep.tile([P, DEGREE, RANK], U8, align_bytes=64)
+
+        u_values = {}
+
+        def regroup_u(n):
+            u_grp = stage.tile([P, RANK, 4], BF16, tag="u_grp", bufs=DEGREE, align_bytes=64)
+            dst = u_grp[:].rearrange("p (c i) t -> p c t i", i=4)
+            src = u_raw[n][:].rearrange("p t (c i) -> p c t i", i=4)
+            if n < DEGREE // 2:
+                nc.scalar.copy(out=dst, in_=src)
+            else:
+                nc.vector.tensor_copy(out=dst, in_=src)
+            u_values[n] = u_grp
+
+        def quantise_u(n):
+            u_grp = u_values[n]
+            nc.vector.quantize_mx(
+                out=u_codes[:, n, :].bitcast(FP8X4),
+                scales=u_scales[:, n, :],
+                in_=u_grp[:].rearrange("p c t -> p (c t)"),
             )
 
         c_codes = keep.tile([P, PIXELS], U32, align_bytes=64)
@@ -277,7 +288,6 @@ def tile_generator_pa_t_kernel(tc, x, U, C, beta, gamma, bn_bias, out):
             )
             h_words[g] = (h_codes, h_scales)
 
-        out_tiles = {}
 
         def stage_two(j):
             h_codes, h_scales = h_words[j // GROUP]
@@ -295,37 +305,45 @@ def tile_generator_pa_t_kernel(tc, x, U, C, beta, gamma, bn_bias, out):
             o_banks[j] = o
 
         def add_beta(j):
-            g = j // GROUP
-            if j % GROUP == 0:
-                out_tiles[g] = work.tile([P, GROUP, PIXELS], F32, tag="out_sb", name="out_sb")
-            out_sb = out_tiles[g]
+            out_sb = work.tile([P, PIXELS], F32, tag="out_sb", bufs=4)
             o = o_banks[j]
             if j % GROUP < GROUP - 1:
                 nc.vector.tensor_tensor(
-                    out=out_sb[:, j % GROUP, :], in0=o[:], in1=beta_bc[:], op=ALU.add
+                    out=out_sb[:], in0=o[:], in1=beta_bc[:], op=ALU.add
                 )
             else:
                 o_sb = work.tile([P, PIXELS], F32, tag="o_sb")
                 nc.scalar.copy(out=o_sb[:], in_=o[:])
                 nc.gpsimd.tensor_tensor(
-                    out=out_sb[:, j % GROUP, :], in0=o_sb[:], in1=beta_bc[:], op=ALU.add
+                    out=out_sb[:], in0=o_sb[:], in1=beta_bc[:], op=ALU.add
                 )
-            if j % GROUP == GROUP - 1:
-                nc.sync.dma_start(
-                    out=out_rows[:, g * GROUP : (g + 1) * GROUP, :], in_=out_sb[:]
-                )
+            nc.sync.dma_start(out=out_rows[:, j, :], in_=out_sb[:])
 
-        prepare_z(0)
-        prepare_z(1)
+        transpose_x(0)
+        normalise(0)
+        regroup_u(0)
+        regroup_u(1)
+        regroup_u(2)
+        quantise_z(0)
+        quantise_u(0)
+        regroup_u(3)
+        quantise_u(1)
+        quantise_u(2)
+        quantise_u(3)
+        for g in range(1, GROUPS):
+            transpose_x(g)
+        normalise(1)
+        for g in range(2, GROUPS):
+            normalise(g)
+            quantise_z(g - 1)
+        quantise_z(GROUPS - 1)
         prepare_c()
-        for step in range(BLOCKS + ADD_LAG + 1):
+        for step in range(BLOCKS + ADD_LAG):
             if step < BLOCKS:
                 stage_one(step)
             g = (step - QUANTISE_LAG) // GROUP
             if (step - QUANTISE_LAG) % GROUP == 0 and 0 <= g < GROUPS:
                 quantise_h(g)
-                if g + 2 < GROUPS:
-                    prepare_z(g + 2)
             if 0 <= step - MATMUL_LAG < BLOCKS:
                 stage_two(step - MATMUL_LAG)
             if 0 <= step - ADD_LAG < BLOCKS:

@@ -10,6 +10,7 @@ U8 = mybir.dt.uint8
 FP8X4 = mybir.dt.float8_e4m3fn_x4
 ACT = mybir.ActivationFunctionType
 ALU = mybir.AluOpType
+AXIS = mybir.AxisListType
 
 P = 128
 BATCH = 4096
@@ -20,14 +21,23 @@ EPS = 1e-5
 BLOCKS = BATCH // P
 GROUP = 4
 GROUPS = BLOCKS // GROUP
+PAIRS = BLOCKS // 2
+PAIR_ROWS = 2 * P
 CHUNKS = RANK // P
-HALF = GROUP // 2
+UNITS = 2 * PAIRS
 COUNT = BATCH * PIXELS
-VECTOR_COUNT = GROUPS * HALF * PIXELS
 
-QUANTISE_LAG = GROUP + 1
-MATMUL_LAG = QUANTISE_LAG + 1
-ADD_LAG = MATMUL_LAG + 1
+VECTOR_BLOCKS = [2, 2, 2, 2, 2, 2, 1, 1]
+SCALAR_BLOCKS = [1, 1, 1, 1, 1, 1, 2, 2]
+VECTOR_TOTAL = sum(VECTOR_BLOCKS)
+
+H_LAG = 3
+VALUE_BUFS = 6
+CODE_BUFS = 6
+C_LAG = 5
+OUT_LAG = 6
+
+TERM_ORDER = (0, 2, 1, 3)
 
 FLOPS = 2 * BATCH * PIXELS * RANK * (DEGREE + 1)
 
@@ -43,260 +53,316 @@ def tile_generator_pa_t_kernel(tc, x, U, C, beta, gamma, bn_bias, out):
         name="stage", bufs=2
     ) as stage, tc.tile_pool(name="work", bufs=3) as work, tc.psum_pool(
         name="psum", bufs=1
-    ) as psum:
-        one_t = const.tile([P, 1], F32)
-        nc.vector.memset(one_t[:], 1.0)
-        warm = const.tile([P, 1], F32)
-        nc.scalar.activation(out=warm[:], in_=one_t[:], func=ACT.Sqrt)
-        ident_f32 = const.tile([P, P], F32)
-        make_identity(nc, ident_f32[:])
-        ident_bf = const.tile([P, P], BF16)
-        make_identity(nc, ident_bf[:])
-        share_bf = const.tile([P, P], BF16)
-        nc.vector.memset(share_bf[:], 1.0 / P)
-        inv_count = const.tile([P, P], F32)
-        nc.vector.memset(inv_count[:], 1.0 / COUNT)
+    ) as psum, tc.manual_schedule():
         gamma_b = const.tile([P, 1], BF16)
         nc.scalar.dma_start(out=gamma_b[:], in_=gamma.partition_broadcast(P))
         bias_b = const.tile([P, 1], BF16)
         nc.scalar.dma_start(out=bias_b[:], in_=bn_bias.partition_broadcast(P))
-
         x_sb = []
         for g in range(GROUPS):
             x_g = keep.tile([P, GROUP, PIXELS], BF16, name="x%d" % g)
             nc.sync.dma_start(out=x_g[:], in_=x_rows[:, g * GROUP : (g + 1) * GROUP, :])
             x_sb.append(x_g)
-        u_raw = []
-        for n in range(DEGREE):
+        u_raw = {}
+        for n in TERM_ORDER:
             u_n = keep.tile([P, 4, RANK], BF16, name="u_raw%d" % n)
             nc.sync.dma_start(
                 out=u_n[:].rearrange("w (u e) c -> w u (e c)", u=2),
                 in_=U[n].rearrange("(u w e) c -> w u (e c)", u=2, e=2),
             )
-            u_raw.append(u_n)
+            u_raw[n] = u_n
         c_raw = keep.tile([P, CHUNKS, RANK], BF16)
         nc.sync.dma_start(out=c_raw[:], in_=C.rearrange("(q p) r -> p q r", p=P))
         beta_bc = const.tile([P, PIXELS], BF16)
         nc.sync.dma_start(out=beta_bc[:], in_=beta.partition_broadcast(P))
 
-        stats = small.tile([P, GROUPS * HALF, 6], F32)
-        squares = small.tile([P, GROUPS], F32)
-        column_sums = psum.tile([P, PIXELS], F32, tag="o", bufs=2)
+        one_t = const.tile([P, 1], F32)
+        nc.vector.memset(one_t[:], 1.0)
+        warm = const.tile([P, 1], F32)
+        nc.scalar.activation(out=warm[:], in_=one_t[:], func=ACT.Abs_reciprocal_sqrt)
+        ones_bf = const.tile([P, 1], BF16)
+        nc.vector.memset(ones_bf[:], 1.0)
+        vector_share = const.tile([P, P], F32)
+        nc.vector.memset(vector_share[:], VECTOR_TOTAL * PIXELS / COUNT)
+        inv_count = const.tile([P, P], F32)
+        nc.vector.memset(inv_count[:], 1.0 / COUNT)
+        ident_f32 = const.tile([P, P], F32)
+        make_identity(nc, ident_f32[:])
+        ident_bf = const.tile([P, P], BF16)
+        make_identity(nc, ident_bf[:])
+
+        xt_banks = {}
+
+        def transpose_x(pair, tag, bufs):
+            xt = psum.tile([P, 2, PAIR_ROWS], F32, tag=tag, bufs=bufs, name="xt")
+            for side in range(2):
+                g, jj = divmod(2 * pair + side, GROUP)
+                words = x_sb[g][:, jj, :].bitcast(F32)
+                for u in range(2):
+                    nc.tensor.transpose(
+                        xt[:, u, side * P : (side + 1) * P],
+                        words[:, u * P : (u + 1) * P],
+                        ident_f32[:],
+                    )
+            xt_banks[pair] = xt
+
+        stats = small.tile([P, VECTOR_TOTAL, 6], F32)
+        squares = small.tile([P, GROUPS + 1], F32)
+        gram = psum.tile([P, P], F32, tag="o", bufs=2)
+        pixel_sums = psum.tile([P, 1], F32, tag="o", bufs=2)
+        seen = 0
         for g in range(GROUPS):
-            for jj in range(HALF):
-                nc.vector.bn_stats(out=stats[:, g * HALF + jj, :], in_=x_sb[g][:, jj, :])
-            unread = stage.tile([P, GROUP - HALF, PIXELS], BF16, tag="unread")
+            v_end = VECTOR_BLOCKS[g]
+            s_end = v_end + SCALAR_BLOCKS[g]
+            for jj in range(v_end):
+                nc.vector.bn_stats(out=stats[:, seen, :], in_=x_sb[g][:, jj, :])
+                seen += 1
+            unread = stage.tile([P, 2, PIXELS], BF16, tag="unread")
             nc.scalar.activation(
-                out=unread[:],
-                in_=x_sb[g][:, HALF:GROUP, :],
+                out=unread[:, : s_end - v_end, :],
+                in_=x_sb[g][:, v_end:s_end, :],
                 func=ACT.Square,
                 accum_out=squares[:, g : g + 1],
             )
-            for jj in range(HALF, GROUP):
-                nc.tensor.matmul(
-                    out=column_sums[:],
-                    lhsT=share_bf[:],
-                    rhs=x_sb[g][:, jj, :],
-                    start=(g == 0 and jj == HALF),
-                    stop=(g == GROUPS - 1 and jj == GROUP - 1),
-                )
-        mean_var = small.tile([P, 2], F32)
-        nc.vector.bn_aggr(out=mean_var[:], in_=stats[:].rearrange("p s d -> p (s d)"))
-        sum_share = small.tile([P, 1], F32)
-        nc.vector.tensor_reduce(
-            out=sum_share[:], in_=column_sums[:], axis=mybir.AxisListType.X, op=ALU.add
-        )
-        square_sum = small.tile([P, 1], F32)
-        nc.vector.tensor_reduce(
-            out=square_sum[:], in_=squares[:], axis=mybir.AxisListType.X, op=ALU.add
-        )
-        second = small.tile([P, 1], F32)
+            for jj in range(v_end, GROUP):
+                for c in range(PIXELS // P):
+                    cols = x_sb[g][:, jj, c * P : (c + 1) * P]
+                    nc.tensor.matmul(
+                        out=pixel_sums[:],
+                        lhsT=cols,
+                        rhs=ones_bf[:],
+                        start=(g == 0 and jj == v_end and c == 0),
+                        stop=(g == GROUPS - 1 and jj == GROUP - 1 and c == PIXELS // P - 1),
+                    )
+                    if jj >= s_end:
+                        nc.tensor.matmul(
+                            out=gram[:],
+                            lhsT=cols,
+                            rhs=cols,
+                            start=(g == 0 and jj == s_end and c == 0),
+                            stop=(g == GROUPS - 1 and jj == GROUP - 1 and c == PIXELS // P - 1),
+                        )
+            if g == 0:
+                transpose_x(0, "odd", 3)
+                transpose_x(1, "odd", 3)
+            elif g == 1:
+                transpose_x(2, "xt", 1)
+
+        u_codes = keep.tile([P, DEGREE, RANK], U32, align_bytes=64)
+        u_scales = keep.tile([P, DEGREE, RANK], U8, align_bytes=64)
+        u_values = {}
+        for n in TERM_ORDER:
+            u_values[n] = keep.tile([P, RANK, 4], BF16, name="u_grp%d" % n, align_bytes=64)
+
+        def regroup_u(engine, n, lo, hi):
+            dst = u_values[n][:, lo:hi, :].rearrange("p (c i) t -> p c t i", i=4)
+            src = u_raw[n][:, :, lo:hi].rearrange("p t (c i) -> p c t i", i=4)
+            if engine == "scalar":
+                nc.scalar.copy(out=dst, in_=src)
+            else:
+                nc.vector.tensor_copy(out=dst, in_=src)
+
+        def quantise_u(n):
+            nc.vector.quantize_mx(
+                out=u_codes[:, n, :].bitcast(FP8X4),
+                scales=u_scales[:, n, :],
+                in_=u_values[n][:].rearrange("p c t -> p (c t)"),
+            )
+
+        half_rank = RANK // 2
+        regroup_u("scalar", 0, half_rank, RANK)
+        vector_part = small.tile([P, 2], F32)
+        nc.vector.bn_aggr(out=vector_part[:], in_=stats[:].rearrange("p s d -> p (s d)"))
         nc.vector.scalar_tensor_tensor(
-            out=second[:], in0=mean_var[:, 0:1], scalar=mean_var[:, 0:1], in1=mean_var[:, 1:2],
-            op0=ALU.mult, op1=ALU.add,
+            out=vector_part[:, 1:2],
+            in0=vector_part[:, 0:1],
+            scalar=vector_part[:, 0:1],
+            in1=vector_part[:, 1:2],
+            op0=ALU.mult,
+            op1=ALU.add,
+        )
+        diagonal = small.tile([P, P], F32)
+        nc.vector.scalar_tensor_tensor(
+            out=diagonal[:],
+            in0=gram[:],
+            scalar=1.0,
+            in1=ident_f32[:],
+            op0=ALU.mult,
+            op1=ALU.mult,
+            accum_out=squares[:, GROUPS : GROUPS + 1],
         )
         sums = small.tile([P, 2], F32)
-        nc.vector.scalar_tensor_tensor(
-            out=sums[:, 0:1], in0=mean_var[:, 0:1], scalar=float(VECTOR_COUNT), in1=sum_share[:],
-            op0=ALU.mult, op1=ALU.add,
-        )
-        nc.vector.scalar_tensor_tensor(
-            out=sums[:, 1:2], in0=second[:], scalar=float(VECTOR_COUNT), in1=square_sum[:],
-            op0=ALU.mult, op1=ALU.add,
-        )
+        nc.vector.tensor_copy(out=sums[:, 0:1], in_=pixel_sums[:])
+        nc.vector.tensor_reduce(out=sums[:, 1:2], in_=squares[:], axis=AXIS.X, op=ALU.add)
         moments_ps = psum.tile([P, 2], F32, tag="o", bufs=2)
-        nc.tensor.matmul(out=moments_ps[:], lhsT=inv_count[:], rhs=sums[:], start=True, stop=True)
-        moments = small.tile([P, 2], F32)
-        nc.vector.tensor_copy(out=moments[:], in_=moments_ps[:])
+        nc.tensor.matmul(
+            out=moments_ps[:], lhsT=vector_share[:], rhs=vector_part[:], start=True, stop=False
+        )
+        nc.tensor.matmul(out=moments_ps[:], lhsT=inv_count[:], rhs=sums[:], start=False, stop=True)
+        regroup_u("vector", 0, 0, half_rank // 2)
+        minus = small.tile([P, 2], F32)
+        nc.vector.tensor_scalar(
+            out=minus[:], in0=moments_ps[:], scalar1=-1.0, scalar2=None, op0=ALU.mult
+        )
         minus_var = small.tile([P, 1], F32)
         nc.vector.scalar_tensor_tensor(
-            out=minus_var[:], in0=moments[:, 0:1], scalar=moments[:, 0:1], in1=moments[:, 1:2],
-            op0=ALU.mult, op1=ALU.subtract,
+            out=minus_var[:],
+            in0=minus[:, 0:1],
+            scalar=minus[:, 0:1],
+            in1=minus[:, 1:2],
+            op0=ALU.mult,
+            op1=ALU.add,
         )
         var_eps = small.tile([P, 1], F32)
         nc.vector.tensor_scalar(
             out=var_eps[:], in0=minus_var[:], scalar1=-1.0, scalar2=EPS, op0=ALU.mult, op1=ALU.add
         )
-        std = small.tile([P, 1], F32)
-        nc.scalar.activation(out=std[:], in_=var_eps[:], func=ACT.Sqrt)
         rstd = small.tile([P, 1], F32)
-        nc.vector.reciprocal(out=rstd[:], in_=std[:])
+        nc.scalar.activation(out=rstd[:], in_=var_eps[:], func=ACT.Abs_reciprocal_sqrt)
+        regroup_u("vector", 0, half_rank // 2, half_rank)
         gain = small.tile([P, 1], F32)
         nc.vector.tensor_tensor(out=gain[:], in0=rstd[:], in1=gamma_b[:], op=ALU.mult)
-        minus_gain = small.tile([P, 1], F32)
-        nc.vector.scalar_tensor_tensor(
-            out=minus_gain[:], in0=rstd[:], scalar=-1.0, in1=gamma_b[:], op0=ALU.mult, op1=ALU.mult
-        )
         shift = small.tile([P, 1], F32)
         nc.vector.scalar_tensor_tensor(
-            out=shift[:], in0=moments[:, 0:1], scalar=minus_gain[:], in1=bias_b[:],
-            op0=ALU.mult, op1=ALU.add,
+            out=shift[:], in0=gain[:], scalar=minus[:, 0:1], in1=bias_b[:], op0=ALU.mult, op1=ALU.add
         )
 
-        xt_words = keep.tile([P, GROUPS, GROUP * P, 2], F32, align_bytes=64)
+        values = {}
+        codes = {}
+        z_at = {}
+        h_at = {}
 
-        def transpose_x(g):
-            for pair in range(GROUP // 2):
-                xt = psum.tile([P, 2, 2 * P], F32, tag="bank", bufs=6)
-                for jj in range(2):
-                    words = x_sb[g][:, 2 * pair + jj, :].bitcast(F32)
-                    for u in range(2):
-                        nc.tensor.transpose(
-                            xt[:, u, jj * P : (jj + 1) * P], words[:, u * P : (u + 1) * P], ident_f32[:]
-                        )
-                nc.scalar.copy(
-                    out=xt_words[:, g, 2 * pair * P : 2 * (pair + 1) * P, :],
-                    in_=xt[:].rearrange("w u c -> w c u"),
+        def open_step(step):
+            values[step] = work.tile(
+                [P, 2, PAIR_ROWS, 2, 2], BF16, tag="values", name="values", bufs=VALUE_BUFS, align_bytes=64
+            )
+            codes[step] = (
+                work.tile([P, 2, PAIR_ROWS], U32, tag="codes", name="codes", bufs=CODE_BUFS, align_bytes=64),
+                work.tile([P, 2, PAIR_ROWS], U8, tag="scales", name="scales", bufs=CODE_BUFS, align_bytes=64),
+            )
+
+        def normalise(engine, pair):
+            dst = values[pair][:, 0, :, :, :]
+            src = xt_banks[pair][:].bitcast(BF16).rearrange("w u (c e) -> w c u e", e=2)
+            if engine == "scalar":
+                nc.scalar.activation(
+                    out=dst, in_=src, func=ACT.Identity, scale=gain[:], bias=shift[:]
+                )
+            else:
+                nc.vector.tensor_scalar(
+                    out=dst, in0=src, scalar1=gain[:], scalar2=shift[:], op0=ALU.mult, op1=ALU.add
                 )
 
-        z_codes = keep.tile([P, GROUPS, GROUP * P], U32, align_bytes=64)
-        z_scales = keep.tile([P, GROUPS, GROUP * P], U8, align_bytes=64)
-        z_values = {}
-
-        def normalise(g):
-            z_grp = stage.tile([P, GROUP * P * 4], BF16, tag="z_grp", bufs=3, align_bytes=64)
-            nc.vector.tensor_scalar(
-                out=z_grp[:],
-                in0=xt_words[:, g, :, :].rearrange("w c u -> w (c u)").bitcast(BF16),
-                scalar1=gain[:],
-                scalar2=shift[:],
-                op0=ALU.mult,
-                op1=ALU.add,
-            )
-            z_values[g] = z_grp
-
-        def quantise_z(g):
+        def quantise(step, lo, hi):
+            step_codes, step_scales = codes[step]
             nc.vector.quantize_mx(
-                out=z_codes[:, g, :].bitcast(FP8X4), scales=z_scales[:, g, :], in_=z_values[g][:]
-            )
-
-        u_codes = keep.tile([P, DEGREE, RANK], U32, align_bytes=64)
-        u_scales = keep.tile([P, DEGREE, RANK], U8, align_bytes=64)
-
-        u_values = {}
-
-        def regroup_u(n):
-            u_grp = stage.tile([P, RANK, 4], BF16, tag="u_grp", bufs=DEGREE, align_bytes=64)
-            dst = u_grp[:].rearrange("p (c i) t -> p c t i", i=4)
-            src = u_raw[n][:].rearrange("p t (c i) -> p c t i", i=4)
-            if n < DEGREE // 2:
-                nc.scalar.copy(out=dst, in_=src)
-            else:
-                nc.vector.tensor_copy(out=dst, in_=src)
-            u_values[n] = u_grp
-
-        def quantise_u(n):
-            u_grp = u_values[n]
-            nc.vector.quantize_mx(
-                out=u_codes[:, n, :].bitcast(FP8X4),
-                scales=u_scales[:, n, :],
-                in_=u_grp[:].rearrange("p c t -> p (c t)"),
+                out=step_codes[:].rearrange("p k b -> p (k b)")[:, lo:hi].bitcast(FP8X4),
+                scales=step_scales[:].rearrange("p k b -> p (k b)")[:, lo:hi],
+                in_=values[step][:].rearrange("p k b h r -> p (k b) (h r)")[:, lo:hi, :].rearrange(
+                    "p b r -> p (b r)"
+                ),
             )
 
         c_codes = keep.tile([P, PIXELS], U32, align_bytes=64)
         c_scales = keep.tile([P, PIXELS], U8, align_bytes=64)
+        c_grp = keep.tile([P, PIXELS, CHUNKS], BF16, align_bytes=64)
+        ct_banks = {}
 
-        def prepare_c():
-            c_grp = keep.tile([P, PIXELS, CHUNKS], BF16, align_bytes=64)
-            for half in range(2):
-                ct = psum.tile([P, CHUNKS, 2 * P], BF16, tag="o", bufs=2)
-                for qq in range(2):
-                    for r in range(CHUNKS):
-                        nc.tensor.transpose(
-                            ct[:, r, qq * P : (qq + 1) * P],
-                            c_raw[:, 2 * half + qq, r * P : (r + 1) * P],
-                            ident_bf[:],
-                        )
-                nc.scalar.copy(
-                    out=c_grp[:, 2 * half * P : 2 * (half + 1) * P, :],
-                    in_=ct[:].rearrange("p r x -> p x r"),
-                )
+        def transpose_c(half):
+            ct = psum.tile([P, CHUNKS, 2 * P], BF16, tag="o", bufs=2)
+            for qq in range(2):
+                for r in range(CHUNKS):
+                    nc.tensor.transpose(
+                        ct[:, r, qq * P : (qq + 1) * P],
+                        c_raw[:, 2 * half + qq, r * P : (r + 1) * P],
+                        ident_bf[:],
+                    )
+            ct_banks[half] = ct
+
+        def copy_c(half):
+            nc.scalar.copy(
+                out=c_grp[:, 2 * half * P : 2 * (half + 1) * P, :],
+                in_=ct_banks[half][:].rearrange("p r x -> p x r"),
+            )
+
+        def quantise_c():
             nc.vector.quantize_mx(
                 out=c_codes[:].bitcast(FP8X4),
                 scales=c_scales[:],
                 in_=c_grp[:].rearrange("p x r -> p (x r)"),
             )
 
-        h_values = {}
-        h_words = {}
+        t_banks = {}
+        t_copies = {}
+        factors = {}
         o_banks = {}
 
-        def stage_one(j):
-            g = j // GROUP
-            cols = slice((j % GROUP) * P, (j % GROUP + 1) * P)
-            t = []
-            for n in range(DEGREE):
-                t_n = psum.tile([P, CHUNKS, P], F32, tag="bank", bufs=6, name="t%d" % n)
-                for r in range(CHUNKS):
-                    ranks = slice(r * P, (r + 1) * P)
-                    nc.tensor.matmul_mx(
-                        out=t_n[:, r, :],
-                        lhsT=u_codes[:, n, ranks].bitcast(FP8X4),
-                        lhsT_scale=u_scales[:, n, ranks],
-                        rhs=z_codes[:, g, cols].bitcast(FP8X4),
-                        rhs_scale=z_scales[:, g, cols],
-                        start=True,
-                        stop=True,
-                    )
-                t.append(t_n[:].rearrange("p r b -> p b r"))
-            t0_sb = work.tile([P, P, CHUNKS], F32, tag="t0_sb")
-            nc.scalar.copy(out=t0_sb[:], in_=t[0])
-            t2_sb = work.tile([P, P, CHUNKS], F32, tag="t2_sb")
-            nc.scalar.activation(out=t2_sb[:], in_=t[2], func=ACT.Copy, bias=1.0)
-            left = work.tile([P, P, CHUNKS], F32, tag="left")
-            nc.vector.scalar_tensor_tensor(
-                out=left[:], in0=t[1], scalar=1.0, in1=t0_sb[:], op0=ALU.add, op1=ALU.mult
+        def multiply_u(unit, n):
+            pair, half = divmod(unit, 2)
+            t_n = psum.tile(
+                [P, 2, PAIR_ROWS],
+                F32,
+                tag="odd" if n % 2 else "even",
+                bufs=3 if n % 2 else 2,
+                name="t",
             )
-            right = work.tile([P, P, CHUNKS], F32, tag="right")
-            nc.vector.scalar_tensor_tensor(
-                out=right[:], in0=t[3], scalar=1.0, in1=t2_sb[:], op0=ALU.add, op1=ALU.mult
-            )
-            if j % GROUP == 0:
-                h_values[g] = work.tile(
-                    [P, GROUP * P, CHUNKS], BF16, tag="h_grp", name="h_grp", align_bytes=64
+            for r in range(2):
+                ranks = slice((2 * half + r) * P, (2 * half + r + 1) * P)
+                nc.tensor.matmul_mx(
+                    out=t_n[:, r, :],
+                    lhsT=u_codes[:, n, ranks].bitcast(FP8X4),
+                    lhsT_scale=u_scales[:, n, ranks],
+                    rhs=codes[pair][0][:, 0, :].bitcast(FP8X4),
+                    rhs_scale=codes[pair][1][:, 0, :],
+                    start=True,
+                    stop=True,
                 )
-            nc.gpsimd.tensor_tensor(out=h_values[g][:, cols, :], in0=left[:], in1=right[:], op=ALU.mult)
+            t_banks[unit, n] = t_n[:].rearrange("p r b -> p b r")
 
-        def quantise_h(g):
-            h_grp = h_values[g]
-            h_codes = work.tile([P, GROUP * P], U32, tag="h_codes", align_bytes=64)
-            h_scales = work.tile([P, GROUP * P], U8, tag="h_scales", align_bytes=64)
-            nc.vector.quantize_mx(
-                out=h_codes[:].bitcast(FP8X4),
-                scales=h_scales[:],
-                in_=h_grp[:].rearrange("p b r -> p (b r)"),
+        def copy_t(unit, n):
+            t_sb = work.tile([P, PAIR_ROWS, 2], F32, tag="t%d_sb" % n, name="t_sb")
+            if n == 0:
+                nc.scalar.copy(out=t_sb[:], in_=t_banks[unit, n])
+            else:
+                nc.scalar.activation(out=t_sb[:], in_=t_banks[unit, n], func=ACT.Copy, bias=1.0)
+            t_copies[unit, n] = t_sb
+
+        def multiply_terms(unit, n):
+            pair, half = divmod(unit, 2)
+            if half == 0:
+                factors[pair, n] = work.tile(
+                    [P, 2, PAIR_ROWS, 2], F32, tag="factor%d" % n, name="factor"
+                )
+            nc.vector.scalar_tensor_tensor(
+                out=factors[pair, n][:, half, :, :],
+                in0=t_banks[unit, n + 1],
+                scalar=1.0,
+                in1=t_copies[unit, n][:],
+                op0=ALU.add,
+                op1=ALU.mult,
             )
-            h_words[g] = (h_codes, h_scales)
 
+        def rows_of(j):
+            return slice((j % 2) * P, (j % 2 + 1) * P)
 
-        def stage_two(j):
-            h_codes, h_scales = h_words[j // GROUP]
-            cols = slice((j % GROUP) * P, (j % GROUP + 1) * P)
-            o = psum.tile([P, PIXELS], F32, tag="o", bufs=2)
+        def multiply_h(engine, j):
+            pair = j // 2
+            rows = rows_of(j)
+            engine.tensor_tensor(
+                out=values[pair + H_LAG][:, 1, rows, :, :],
+                in0=factors[pair, 0][:, :, rows, :].rearrange("p h b r -> p b h r"),
+                in1=factors[pair, 2][:, :, rows, :].rearrange("p h b r -> p b h r"),
+                op=ALU.mult,
+            )
+
+        def multiply_c(j, tag="o", bufs=2):
+            h_codes, h_scales = codes[j // 2 + H_LAG]
+            rows = rows_of(j)
+            o = psum.tile([P, PIXELS], F32, tag=tag, bufs=bufs, name="o")
             nc.tensor.matmul_mx(
                 out=o[:],
-                lhsT=h_codes[:, cols].bitcast(FP8X4),
-                lhsT_scale=h_scales[:, cols],
+                lhsT=h_codes[:, 1, rows].bitcast(FP8X4),
+                lhsT_scale=h_scales[:, 1, rows],
                 rhs=c_codes[:].bitcast(FP8X4),
                 rhs_scale=c_scales[:],
                 start=True,
@@ -304,47 +370,81 @@ def tile_generator_pa_t_kernel(tc, x, U, C, beta, gamma, bn_bias, out):
             )
             o_banks[j] = o
 
-        def add_beta(j):
-            out_sb = work.tile([P, PIXELS], F32, tag="out_sb", bufs=4)
+        def add_beta(j, shared):
+            out_sb = work.tile([P, PIXELS], F32, tag="out_sb", bufs=8)
             o = o_banks[j]
-            if j % GROUP < GROUP - 1:
-                nc.vector.tensor_tensor(
-                    out=out_sb[:], in0=o[:], in1=beta_bc[:], op=ALU.add
-                )
-            else:
+            if shared:
                 o_sb = work.tile([P, PIXELS], F32, tag="o_sb")
                 nc.scalar.copy(out=o_sb[:], in_=o[:])
-                nc.gpsimd.tensor_tensor(
-                    out=out_sb[:], in0=o_sb[:], in1=beta_bc[:], op=ALU.add
-                )
+                nc.gpsimd.tensor_tensor(out=out_sb[:], in0=o_sb[:], in1=beta_bc[:], op=ALU.add)
+            else:
+                nc.vector.tensor_tensor(out=out_sb[:], in0=o[:], in1=beta_bc[:], op=ALU.add)
             nc.sync.dma_start(out=out_rows[:, j, :], in_=out_sb[:])
 
-        transpose_x(0)
-        normalise(0)
-        regroup_u(0)
-        regroup_u(1)
-        regroup_u(2)
-        quantise_z(0)
+        for step in range(H_LAG):
+            open_step(step)
+        normalise("vector", 0)
+        normalise("vector", 1)
+        quantise(0, 0, PAIR_ROWS)
+        regroup_u("scalar", 2, 0, RANK)
+        regroup_u("scalar", 1, 0, RANK)
         quantise_u(0)
-        regroup_u(3)
-        quantise_u(1)
+        quantise(1, 0, PAIR_ROWS)
         quantise_u(2)
+        regroup_u("vector", 3, 0, RANK)
+        quantise_u(1)
         quantise_u(3)
-        for g in range(1, GROUPS):
-            transpose_x(g)
-        normalise(1)
-        for g in range(2, GROUPS):
-            normalise(g)
-            quantise_z(g - 1)
-        quantise_z(GROUPS - 1)
-        prepare_c()
-        for step in range(BLOCKS + ADD_LAG):
-            if step < BLOCKS:
-                stage_one(step)
-            g = (step - QUANTISE_LAG) // GROUP
-            if (step - QUANTISE_LAG) % GROUP == 0 and 0 <= g < GROUPS:
-                quantise_h(g)
-            if 0 <= step - MATMUL_LAG < BLOCKS:
-                stage_two(step - MATMUL_LAG)
-            if 0 <= step - ADD_LAG < BLOCKS:
-                add_beta(step - ADD_LAG)
+
+        shared_blocks = (0, 4)
+
+        def multiply_even(unit):
+            for n in (0, 2):
+                multiply_u(unit, n)
+                copy_t(unit, n)
+
+        multiply_even(0)
+        for unit in range(UNITS):
+            pair, half = divmod(unit, 2)
+            j_c = unit - C_LAG
+            j_out = unit - OUT_LAG
+            if half == 0:
+                open_step(pair + H_LAG)
+                if pair + 2 < PAIRS:
+                    normalise("scalar", pair + 2)
+            if unit + 1 < UNITS:
+                multiply_even(unit + 1)
+            for n in (1, 3):
+                multiply_u(unit, n)
+            if half == 0 and pair + 3 < PAIRS:
+                transpose_x(pair + 3, "xt", 1)
+            if unit in (1, 2):
+                transpose_c(unit - 1)
+                copy_c(unit - 1)
+            if j_out >= 0:
+                add_beta(j_out, j_out % 8 in shared_blocks)
+            if j_c >= 0:
+                multiply_c(j_c)
+            multiply_terms(unit, 0)
+            multiply_terms(unit, 2)
+            if half == 1:
+                first = 0 if pair + 2 < PAIRS else PAIR_ROWS
+                last = 2 * PAIR_ROWS if pair + 2 >= H_LAG else PAIR_ROWS
+                quantise(pair + 2, first, last)
+            if unit == 2:
+                quantise_c()
+            if half == 1 and pair < PAIRS - 1:
+                multiply_h(nc.gpsimd, 2 * pair)
+                multiply_h(nc.gpsimd, 2 * pair + 1)
+
+        def tail_bank(j):
+            return ("even", 2) if j % 2 else ("odd", 3)
+
+        multiply_h(nc.gpsimd, BLOCKS - 2)
+        multiply_h(nc.vector, BLOCKS - 1)
+        multiply_c(BLOCKS - C_LAG)
+        for j in range(BLOCKS - OUT_LAG, BLOCKS):
+            if j == BLOCKS - OUT_LAG + 1:
+                quantise(PAIRS - 1 + H_LAG, PAIR_ROWS, 2 * PAIR_ROWS)
+            if j + OUT_LAG - C_LAG + 1 < BLOCKS:
+                multiply_c(j + OUT_LAG - C_LAG + 1, *tail_bank(j))
+            add_beta(j, j % 2 == 1 and j < BLOCKS - 1)

@@ -24,7 +24,6 @@ GROUPS = BLOCKS // GROUP
 PAIRS = BLOCKS // 2
 PAIR_ROWS = 2 * P
 CHUNKS = RANK // P
-UNITS = 2 * PAIRS
 COUNT = BATCH * PIXELS
 
 VECTOR_BLOCKS = [2, 2, 2, 2, 2, 2, 1, 1]
@@ -234,7 +233,7 @@ def tile_generator_pa_t_kernel(tc, x, U, C, beta, gamma, bn_bias, out):
 
         def open_step(step):
             values[step] = work.tile(
-                [P, 2, PAIR_ROWS, 2, 2], BF16, tag="values", name="values", bufs=VALUE_BUFS, align_bytes=64
+                [P, 2, PAIR_ROWS, CHUNKS], BF16, tag="values", name="values", bufs=VALUE_BUFS, align_bytes=64
             )
             codes[step] = (
                 work.tile([P, 2, PAIR_ROWS], U32, tag="codes", name="codes", bufs=CODE_BUFS, align_bytes=64),
@@ -242,7 +241,7 @@ def tile_generator_pa_t_kernel(tc, x, U, C, beta, gamma, bn_bias, out):
             )
 
         def normalise(engine, pair):
-            dst = values[pair][:, 0, :, :, :]
+            dst = values[pair][:, 0, :, :].rearrange("w c (u e) -> w c u e", e=2)
             src = xt_banks[pair][:].bitcast(BF16).rearrange("w u (c e) -> w c u e", e=2)
             if engine == "scalar":
                 nc.scalar.activation(
@@ -258,9 +257,7 @@ def tile_generator_pa_t_kernel(tc, x, U, C, beta, gamma, bn_bias, out):
             nc.vector.quantize_mx(
                 out=step_codes[:].rearrange("p k b -> p (k b)")[:, lo:hi].bitcast(FP8X4),
                 scales=step_scales[:].rearrange("p k b -> p (k b)")[:, lo:hi],
-                in_=values[step][:].rearrange("p k b h r -> p (k b) (h r)")[:, lo:hi, :].rearrange(
-                    "p b r -> p (b r)"
-                ),
+                in_=values[step][:].rearrange("p k b r -> p (k b r)")[:, CHUNKS * lo : CHUNKS * hi],
             )
 
         c_codes = keep.tile([P, PIXELS], U32, align_bytes=64)
@@ -297,61 +294,57 @@ def tile_generator_pa_t_kernel(tc, x, U, C, beta, gamma, bn_bias, out):
         factors = {}
         o_banks = {}
 
-        def multiply_u(unit, n):
-            pair, half = divmod(unit, 2)
+        def rows_of(j):
+            return slice((j % 2) * P, (j % 2 + 1) * P)
+
+        def multiply_u(j, n):
+            z_codes, z_scales = codes[j // 2]
+            rows = rows_of(j)
             t_n = psum.tile(
-                [P, 2, PAIR_ROWS],
+                [P, CHUNKS, P],
                 F32,
                 tag="odd" if n % 2 else "even",
                 bufs=3 if n % 2 else 2,
                 name="t",
             )
-            for r in range(2):
-                ranks = slice((2 * half + r) * P, (2 * half + r + 1) * P)
+            for r in range(CHUNKS):
+                ranks = slice(r * P, (r + 1) * P)
                 nc.tensor.matmul_mx(
                     out=t_n[:, r, :],
                     lhsT=u_codes[:, n, ranks].bitcast(FP8X4),
                     lhsT_scale=u_scales[:, n, ranks],
-                    rhs=codes[pair][0][:, 0, :].bitcast(FP8X4),
-                    rhs_scale=codes[pair][1][:, 0, :],
+                    rhs=z_codes[:, 0, rows].bitcast(FP8X4),
+                    rhs_scale=z_scales[:, 0, rows],
                     start=True,
                     stop=True,
                 )
-            t_banks[unit, n] = t_n[:].rearrange("p r b -> p b r")
+            t_banks[j, n] = t_n[:].rearrange("p r b -> p b r")
 
-        def copy_t(unit, n):
-            t_sb = work.tile([P, PAIR_ROWS, 2], F32, tag="t%d_sb" % n, name="t_sb")
+        def copy_t(j, n):
+            t_sb = work.tile([P, P, CHUNKS], F32, tag="t%d_sb" % n, name="t_sb")
             if n == 0:
-                nc.scalar.copy(out=t_sb[:], in_=t_banks[unit, n])
+                nc.scalar.copy(out=t_sb[:], in_=t_banks[j, n])
             else:
-                nc.scalar.activation(out=t_sb[:], in_=t_banks[unit, n], func=ACT.Copy, bias=1.0)
-            t_copies[unit, n] = t_sb
+                nc.scalar.activation(out=t_sb[:], in_=t_banks[j, n], func=ACT.Copy, bias=1.0)
+            t_copies[j, n] = t_sb
 
-        def multiply_terms(unit, n):
-            pair, half = divmod(unit, 2)
-            if half == 0:
-                factors[pair, n] = work.tile(
-                    [P, 2, PAIR_ROWS, 2], F32, tag="factor%d" % n, name="factor"
-                )
+        def multiply_terms(j, n):
+            factor = work.tile([P, P, CHUNKS], F32, tag="factor%d" % n, name="factor")
             nc.vector.scalar_tensor_tensor(
-                out=factors[pair, n][:, half, :, :],
-                in0=t_banks[unit, n + 1],
+                out=factor[:],
+                in0=t_banks[j, n + 1],
                 scalar=1.0,
-                in1=t_copies[unit, n][:],
+                in1=t_copies[j, n][:],
                 op0=ALU.add,
                 op1=ALU.mult,
             )
-
-        def rows_of(j):
-            return slice((j % 2) * P, (j % 2 + 1) * P)
+            factors[j, n] = factor
 
         def multiply_h(engine, j):
-            pair = j // 2
-            rows = rows_of(j)
             engine.tensor_tensor(
-                out=values[pair + H_LAG][:, 1, rows, :, :],
-                in0=factors[pair, 0][:, :, rows, :].rearrange("p h b r -> p b h r"),
-                in1=factors[pair, 2][:, :, rows, :].rearrange("p h b r -> p b h r"),
+                out=values[j // 2 + H_LAG][:, 1, rows_of(j), :],
+                in0=factors[j, 0][:],
+                in1=factors[j, 2][:],
                 op=ALU.mult,
             )
 
@@ -395,52 +388,46 @@ def tile_generator_pa_t_kernel(tc, x, U, C, beta, gamma, bn_bias, out):
         quantise_u(1)
         quantise_u(3)
 
-        shared_blocks = (0, 4)
+        shared_blocks = (3, 7)
 
-        def multiply_even(unit):
+        def multiply_even(j):
             for n in (0, 2):
-                multiply_u(unit, n)
-                copy_t(unit, n)
+                multiply_u(j, n)
+                copy_t(j, n)
 
         multiply_even(0)
-        for unit in range(UNITS):
-            pair, half = divmod(unit, 2)
-            j_c = unit - C_LAG
-            j_out = unit - OUT_LAG
+        for j in range(BLOCKS):
+            pair, half = divmod(j, 2)
             if half == 0:
                 open_step(pair + H_LAG)
                 if pair + 2 < PAIRS:
                     normalise("scalar", pair + 2)
-            if unit + 1 < UNITS:
-                multiply_even(unit + 1)
+            if j + 1 < BLOCKS:
+                multiply_even(j + 1)
             for n in (1, 3):
-                multiply_u(unit, n)
+                multiply_u(j, n)
             if half == 0 and pair + 3 < PAIRS:
                 transpose_x(pair + 3, "xt", 1)
-            if unit in (1, 2):
-                transpose_c(unit - 1)
-                copy_c(unit - 1)
-            if j_out >= 0:
-                add_beta(j_out, j_out % 8 in shared_blocks)
-            if j_c >= 0:
-                multiply_c(j_c)
-            multiply_terms(unit, 0)
-            multiply_terms(unit, 2)
+            if j in (1, 2):
+                transpose_c(j - 1)
+                copy_c(j - 1)
+            if j >= OUT_LAG:
+                add_beta(j - OUT_LAG, (j - OUT_LAG) % 8 in shared_blocks)
+            if j >= C_LAG:
+                multiply_c(j - C_LAG)
+            multiply_terms(j, 0)
+            multiply_terms(j, 2)
             if half == 1:
                 first = 0 if pair + 2 < PAIRS else PAIR_ROWS
                 last = 2 * PAIR_ROWS if pair + 2 >= H_LAG else PAIR_ROWS
                 quantise(pair + 2, first, last)
-            if unit == 2:
+            if j == 2:
                 quantise_c()
-            if half == 1 and pair < PAIRS - 1:
-                multiply_h(nc.gpsimd, 2 * pair)
-                multiply_h(nc.gpsimd, 2 * pair + 1)
+            multiply_h(nc.vector if j == BLOCKS - 1 else nc.gpsimd, j)
 
         def tail_bank(j):
             return ("even", 2) if j % 2 else ("odd", 3)
 
-        multiply_h(nc.gpsimd, BLOCKS - 2)
-        multiply_h(nc.vector, BLOCKS - 1)
         multiply_c(BLOCKS - C_LAG)
         for j in range(BLOCKS - OUT_LAG, BLOCKS):
             if j == BLOCKS - OUT_LAG + 1:

@@ -53,10 +53,12 @@ def tile_generator_pa_t_kernel(tc, x, U, C, beta, gamma, bn_bias, out):
     ) as stage, tc.tile_pool(name="work", bufs=3) as work, tc.psum_pool(
         name="psum", bufs=1
     ) as psum, tc.manual_schedule():
-        gamma_b = const.tile([P, 1], BF16)
-        nc.scalar.dma_start(out=gamma_b[:], in_=gamma.partition_broadcast(P))
-        bias_b = const.tile([P, 1], BF16)
-        nc.scalar.dma_start(out=bias_b[:], in_=bn_bias.partition_broadcast(P))
+        affine_rows = []
+        for vector in (gamma, bn_bias):
+            row = const.tile([P, 2], BF16, name="row%d" % len(affine_rows))
+            nc.vector.memset(row[:], 0.0)
+            nc.scalar.dma_start(out=row[0:1, 0:1], in_=vector.rearrange("(a b) -> a b", a=1))
+            affine_rows.append(row)
         x_sb = []
         for g in range(GROUPS):
             x_g = keep.tile([P, GROUP, PIXELS], BF16, name="x%d" % g)
@@ -79,7 +81,7 @@ def tile_generator_pa_t_kernel(tc, x, U, C, beta, gamma, bn_bias, out):
         nc.vector.memset(one_t[:], 1.0)
         warm = const.tile([P, 1], F32)
         nc.scalar.activation(out=warm[:], in_=one_t[:], func=ACT.Abs_reciprocal_sqrt)
-        ones_bf = const.tile([P, 1], BF16)
+        ones_bf = const.tile([P, P], BF16)
         nc.vector.memset(ones_bf[:], 1.0)
         vector_share = const.tile([P, P], F32)
         nc.vector.memset(vector_share[:], VECTOR_TOTAL * PIXELS / COUNT)
@@ -89,6 +91,27 @@ def tile_generator_pa_t_kernel(tc, x, U, C, beta, gamma, bn_bias, out):
         make_identity(nc, ident_f32[:])
         ident_bf = const.tile([P, P], BF16)
         make_identity(nc, ident_bf[:])
+
+        u_codes = keep.tile([P, DEGREE, RANK], U32, align_bytes=64)
+        u_scales = keep.tile([P, DEGREE, RANK], U8, align_bytes=64)
+        u_values = {}
+        for n in TERM_ORDER:
+            u_values[n] = keep.tile([P, RANK, 4], BF16, name="u_grp%d" % n, align_bytes=64)
+
+        def regroup_u(engine, n, lo, hi):
+            dst = u_values[n][:, lo:hi, :].rearrange("p (c i) t -> p c t i", i=4)
+            src = u_raw[n][:, :, lo:hi].rearrange("p t (c i) -> p c t i", i=4)
+            if engine == "scalar":
+                nc.scalar.copy(out=dst, in_=src)
+            else:
+                nc.vector.tensor_copy(out=dst, in_=src)
+
+        def quantise_u(n):
+            nc.vector.quantize_mx(
+                out=u_codes[:, n, :].bitcast(FP8X4),
+                scales=u_scales[:, n, :],
+                in_=u_values[n][:].rearrange("p c t -> p (c t)"),
+            )
 
         xt_banks = {}
 
@@ -129,7 +152,7 @@ def tile_generator_pa_t_kernel(tc, x, U, C, beta, gamma, bn_bias, out):
                     nc.tensor.matmul(
                         out=pixel_sums[:],
                         lhsT=cols,
-                        rhs=ones_bf[:],
+                        rhs=ones_bf[:, 0:1],
                         start=(g == 0 and jj == v_end and c == 0),
                         stop=(g == GROUPS - 1 and jj == GROUP - 1 and c == PIXELS // P - 1),
                     )
@@ -147,27 +170,6 @@ def tile_generator_pa_t_kernel(tc, x, U, C, beta, gamma, bn_bias, out):
             elif g == 1:
                 transpose_x(2, "xt", 1)
 
-        u_codes = keep.tile([P, DEGREE, RANK], U32, align_bytes=64)
-        u_scales = keep.tile([P, DEGREE, RANK], U8, align_bytes=64)
-        u_values = {}
-        for n in TERM_ORDER:
-            u_values[n] = keep.tile([P, RANK, 4], BF16, name="u_grp%d" % n, align_bytes=64)
-
-        def regroup_u(engine, n, lo, hi):
-            dst = u_values[n][:, lo:hi, :].rearrange("p (c i) t -> p c t i", i=4)
-            src = u_raw[n][:, :, lo:hi].rearrange("p t (c i) -> p c t i", i=4)
-            if engine == "scalar":
-                nc.scalar.copy(out=dst, in_=src)
-            else:
-                nc.vector.tensor_copy(out=dst, in_=src)
-
-        def quantise_u(n):
-            nc.vector.quantize_mx(
-                out=u_codes[:, n, :].bitcast(FP8X4),
-                scales=u_scales[:, n, :],
-                in_=u_values[n][:].rearrange("p c t -> p (c t)"),
-            )
-
         half_rank = RANK // 2
         regroup_u("scalar", 0, half_rank, RANK)
         vector_part = small.tile([P, 2], F32)
@@ -180,6 +182,11 @@ def tile_generator_pa_t_kernel(tc, x, U, C, beta, gamma, bn_bias, out):
             op0=ALU.mult,
             op1=ALU.add,
         )
+        affine_ps = psum.tile([P, 2, 2], F32, tag="even", bufs=2)
+        for k in range(2):
+            nc.tensor.matmul(
+                out=affine_ps[:, k, :], lhsT=ones_bf[:], rhs=affine_rows[k][:], start=True, stop=True
+            )
         diagonal = small.tile([P, P], F32)
         nc.vector.scalar_tensor_tensor(
             out=diagonal[:],
@@ -199,6 +206,8 @@ def tile_generator_pa_t_kernel(tc, x, U, C, beta, gamma, bn_bias, out):
         )
         nc.tensor.matmul(out=moments_ps[:], lhsT=inv_count[:], rhs=sums[:], start=False, stop=True)
         regroup_u("vector", 0, 0, half_rank // 2)
+        affine = small.tile([P, 2, 2], F32)
+        nc.vector.tensor_copy(out=affine[:], in_=affine_ps[:])
         minus = small.tile([P, 2], F32)
         nc.vector.tensor_scalar(
             out=minus[:], in0=moments_ps[:], scalar1=-1.0, scalar2=None, op0=ALU.mult
@@ -212,18 +221,25 @@ def tile_generator_pa_t_kernel(tc, x, U, C, beta, gamma, bn_bias, out):
             op0=ALU.mult,
             op1=ALU.add,
         )
-        var_eps = small.tile([P, 1], F32)
-        nc.vector.tensor_scalar(
-            out=var_eps[:], in0=minus_var[:], scalar1=-1.0, scalar2=EPS, op0=ALU.mult, op1=ALU.add
+        minus_product = small.tile([P, 1], F32)
+        nc.vector.tensor_tensor(
+            out=minus_product[:], in0=minus[:, 0:1], in1=affine[:, 0, 0:1], op=ALU.mult
         )
         rstd = small.tile([P, 1], F32)
-        nc.scalar.activation(out=rstd[:], in_=var_eps[:], func=ACT.Abs_reciprocal_sqrt)
+        nc.scalar.activation(
+            out=rstd[:], in_=minus_var[:], func=ACT.Abs_reciprocal_sqrt, scale=-1.0, bias=EPS
+        )
         regroup_u("vector", 0, half_rank // 2, half_rank)
         gain = small.tile([P, 1], F32)
-        nc.vector.tensor_tensor(out=gain[:], in0=rstd[:], in1=gamma_b[:], op=ALU.mult)
+        nc.vector.tensor_tensor(out=gain[:], in0=rstd[:], in1=affine[:, 0, 0:1], op=ALU.mult)
         shift = small.tile([P, 1], F32)
         nc.vector.scalar_tensor_tensor(
-            out=shift[:], in0=gain[:], scalar=minus[:, 0:1], in1=bias_b[:], op0=ALU.mult, op1=ALU.add
+            out=shift[:],
+            in0=rstd[:],
+            scalar=minus_product[:],
+            in1=affine[:, 1, 0:1],
+            op0=ALU.mult,
+            op1=ALU.add,
         )
 
         values = {}
@@ -408,9 +424,9 @@ def tile_generator_pa_t_kernel(tc, x, U, C, beta, gamma, bn_bias, out):
                 multiply_u(j, n)
             if half == 0 and pair + 3 < PAIRS:
                 transpose_x(pair + 3, "xt", 1)
-            if j in (1, 2):
-                transpose_c(j - 1)
-                copy_c(j - 1)
+            if j in (2, 2 + 1):
+                transpose_c(j - 2)
+                copy_c(j - 2)
             if j >= OUT_LAG:
                 add_beta(j - OUT_LAG, (j - OUT_LAG) % 8 in shared_blocks)
             if j >= C_LAG:
@@ -421,7 +437,7 @@ def tile_generator_pa_t_kernel(tc, x, U, C, beta, gamma, bn_bias, out):
                 first = 0 if pair + 2 < PAIRS else PAIR_ROWS
                 last = 2 * PAIR_ROWS if pair + 2 >= H_LAG else PAIR_ROWS
                 quantise(pair + 2, first, last)
-            if j == 2:
+            if j == 4:
                 quantise_c()
             multiply_h(nc.vector if j == BLOCKS - 1 else nc.gpsimd, j)
 

@@ -26,8 +26,8 @@ PAIR_ROWS = 2 * P
 CHUNKS = RANK // P
 COUNT = BATCH * PIXELS
 
-VECTOR_BLOCKS = [2, 2, 2, 2, 2, 2, 1, 1]
-SCALAR_BLOCKS = [1, 1, 1, 1, 1, 1, 2, 2]
+VECTOR_BLOCKS = [2, 2, 1, 2, 2, 2, 1, 1]
+SCALAR_BLOCKS = [1, 1, 1, 1, 1, 1, 2, 1]
 VECTOR_TOTAL = sum(VECTOR_BLOCKS)
 
 H_LAG = 3
@@ -416,30 +416,46 @@ def tile_generator_pa_t_kernel(tc, x, U, C, beta, gamma, bn_bias, out):
             pair, half = divmod(j, 2)
             if half == 0:
                 open_step(pair + H_LAG)
+                if j + 1 < BLOCKS:
+                    multiply_even(j + 1)
+                for n in (1, 3):
+                    multiply_u(j, n)
                 if pair + 2 < PAIRS:
-                    normalise("scalar", pair + 2)
-            if j + 1 < BLOCKS:
-                multiply_even(j + 1)
-            for n in (1, 3):
-                multiply_u(j, n)
-            if half == 0 and pair + 3 < PAIRS:
-                transpose_x(pair + 3, "xt", 1)
-            if j in (2, 2 + 1):
-                transpose_c(j - 2)
-                copy_c(j - 2)
-            if j >= OUT_LAG:
-                add_beta(j - OUT_LAG, (j - OUT_LAG) % 8 in shared_blocks)
-            if j >= C_LAG:
-                multiply_c(j - C_LAG)
-            multiply_terms(j, 0)
-            multiply_terms(j, 2)
-            if half == 1:
+                    normalise("vector" if pair < 2 else "scalar", pair + 2)
+                if j in (2, 2 + 1):
+                    transpose_c(j - 2)
+                    copy_c(j - 2)
+                if j >= OUT_LAG:
+                    add_beta(j - OUT_LAG, (j - OUT_LAG) % 8 in shared_blocks)
+                if j >= C_LAG:
+                    multiply_c(j - C_LAG)
+                multiply_terms(j, 0)
+                multiply_terms(j, 2)
+                if j == 4:
+                    quantise_c()
+                multiply_h(nc.vector if j == BLOCKS - 1 else nc.gpsimd, j)
+            else:
+                if j + 1 < BLOCKS:
+                    multiply_even(j + 1)
+                for n in (1, 3):
+                    multiply_u(j, n)
+                if pair + 3 < PAIRS:
+                    transpose_x(pair + 3, "xt", 1)
+                if j in (2, 2 + 1):
+                    transpose_c(j - 2)
+                    copy_c(j - 2)
+                if j >= OUT_LAG:
+                    add_beta(j - OUT_LAG, (j - OUT_LAG) % 8 in shared_blocks)
+                if j >= C_LAG:
+                    multiply_c(j - C_LAG)
+                multiply_terms(j, 0)
+                multiply_terms(j, 2)
                 first = 0 if pair + 2 < PAIRS else PAIR_ROWS
                 last = 2 * PAIR_ROWS if pair + 2 >= H_LAG else PAIR_ROWS
                 quantise(pair + 2, first, last)
-            if j == 4:
-                quantise_c()
-            multiply_h(nc.vector if j == BLOCKS - 1 else nc.gpsimd, j)
+                if j == 4:
+                    quantise_c()
+                multiply_h(nc.vector if j == BLOCKS - 1 else nc.gpsimd, j)
 
         def tail_bank(j):
             return ("even", 2) if j % 2 else ("odd", 3)

@@ -26,9 +26,10 @@ PAIR_ROWS = 2 * P
 CHUNKS = RANK // P
 COUNT = BATCH * PIXELS
 
-VECTOR_BLOCKS = [2, 2, 1, 2, 2, 2, 1, 1]
-SCALAR_BLOCKS = [1, 1, 1, 1, 1, 1, 2, 1]
+VECTOR_BLOCKS = [2, 2, 2, 2, 2, 2, 1, 0]
+SCALAR_BLOCKS = [1, 1, 1, 1, 1, 1, 1, 2]
 VECTOR_TOTAL = sum(VECTOR_BLOCKS)
+SCALAR_TOTAL = sum(SCALAR_BLOCKS)
 
 H_LAG = 3
 VALUE_BUFS = 6
@@ -95,6 +96,7 @@ def tile_generator_pa_t_kernel(tc, x, U, C, beta, gamma, bn_bias, out):
         u_codes = keep.tile([P, DEGREE, RANK], U32, align_bytes=64)
         u_scales = keep.tile([P, DEGREE, RANK], U8, align_bytes=64)
         u_values = {}
+
         for n in TERM_ORDER:
             u_values[n] = keep.tile([P, RANK, 4], BF16, name="u_grp%d" % n, align_bytes=64)
 
@@ -105,6 +107,21 @@ def tile_generator_pa_t_kernel(tc, x, U, C, beta, gamma, bn_bias, out):
                 nc.scalar.copy(out=dst, in_=src)
             else:
                 nc.vector.tensor_copy(out=dst, in_=src)
+
+        def spread_u(n):
+            for ranks in (slice(0, RANK // 2), slice(RANK // 2, RANK)):
+                grouped = psum.tile(
+                    [P, RANK // 2, 4], BF16, tag="o" if ranks.start else "even", bufs=2, name="grouped"
+                )
+                for u in range(2):
+                    nc.tensor.matmul(
+                        out=grouped[:, :, 2 * u : 2 * u + 2],
+                        lhsT=ident_bf[:],
+                        rhs=u_raw[n][:, 2 * u : 2 * u + 2, ranks].rearrange("w e c -> w c e"),
+                        start=True,
+                        stop=True,
+                    )
+                nc.scalar.copy(out=u_values[n][:, ranks, :], in_=grouped[:])
 
         def quantise_u(n):
             nc.vector.quantize_mx(
@@ -129,23 +146,54 @@ def tile_generator_pa_t_kernel(tc, x, U, C, beta, gamma, bn_bias, out):
             xt_banks[pair] = xt
 
         stats = small.tile([P, VECTOR_TOTAL, 6], F32)
-        squares = small.tile([P, GROUPS + 1], F32)
+        squares = small.tile([P, SCALAR_TOTAL], F32)
         gram = psum.tile([P, P], F32, tag="o", bufs=2)
         pixel_sums = psum.tile([P, 1], F32, tag="o", bufs=2)
-        seen = 0
+        v_seen = 0
+        s_seen = 0
         for g in range(GROUPS):
+            last_group = g == GROUPS - 1
             v_end = VECTOR_BLOCKS[g]
             s_end = v_end + SCALAR_BLOCKS[g]
             for jj in range(v_end):
-                nc.vector.bn_stats(out=stats[:, seen, :], in_=x_sb[g][:, jj, :])
-                seen += 1
-            unread = stage.tile([P, 2, PIXELS], BF16, tag="unread")
-            nc.scalar.activation(
-                out=unread[:, : s_end - v_end, :],
-                in_=x_sb[g][:, v_end:s_end, :],
-                func=ACT.Square,
-                accum_out=squares[:, g : g + 1],
-            )
+                nc.vector.bn_stats(out=stats[:, v_seen, :], in_=x_sb[g][:, jj, :])
+                v_seen += 1
+            for jj in range(v_end, s_end):
+                unread = stage.tile([P, PIXELS], BF16, tag="unread")
+                nc.scalar.activation(
+                    out=unread[:],
+                    in_=x_sb[g][:, jj, :],
+                    func=ACT.Square,
+                    accum_out=squares[:, s_seen : s_seen + 1],
+                )
+                s_seen += 1
+            if last_group:
+                vector_part = small.tile([P, 2], F32)
+                nc.vector.bn_aggr(out=vector_part[:], in_=stats[:].rearrange("p s d -> p (s d)"))
+                nc.vector.scalar_tensor_tensor(
+                    out=vector_part[:, 1:2],
+                    in0=vector_part[:, 0:1],
+                    scalar=vector_part[:, 0:1],
+                    in1=vector_part[:, 1:2],
+                    op0=ALU.mult,
+                    op1=ALU.add,
+                )
+                early = SCALAR_TOTAL - SCALAR_BLOCKS[g]
+                early_squares = small.tile([P, 1], F32)
+                nc.vector.tensor_reduce(
+                    out=early_squares[:], in_=squares[:, :early], axis=AXIS.X, op=ALU.add
+                )
+                affine_ps = psum.tile([P, 2, 2], F32, tag="odd", bufs=3)
+                for k in range(2):
+                    nc.tensor.matmul(
+                        out=affine_ps[:, k, :],
+                        lhsT=ones_bf[:],
+                        rhs=affine_rows[k][:],
+                        start=True,
+                        stop=True,
+                    )
+                affine = small.tile([P, 2, 2], F32)
+                nc.vector.tensor_copy(out=affine[:], in_=affine_ps[:])
             for jj in range(v_end, GROUP):
                 for c in range(PIXELS // P):
                     cols = x_sb[g][:, jj, c * P : (c + 1) * P]
@@ -154,7 +202,7 @@ def tile_generator_pa_t_kernel(tc, x, U, C, beta, gamma, bn_bias, out):
                         lhsT=cols,
                         rhs=ones_bf[:, 0:1],
                         start=(g == 0 and jj == v_end and c == 0),
-                        stop=(g == GROUPS - 1 and jj == GROUP - 1 and c == PIXELS // P - 1),
+                        stop=(last_group and jj == GROUP - 1 and c == PIXELS // P - 1),
                     )
                     if jj >= s_end:
                         nc.tensor.matmul(
@@ -162,7 +210,7 @@ def tile_generator_pa_t_kernel(tc, x, U, C, beta, gamma, bn_bias, out):
                             lhsT=cols,
                             rhs=cols,
                             start=(g == 0 and jj == s_end and c == 0),
-                            stop=(g == GROUPS - 1 and jj == GROUP - 1 and c == PIXELS // P - 1),
+                            stop=(last_group and jj == GROUP - 1 and c == PIXELS // P - 1),
                         )
             if g == 0:
                 transpose_x(0, "odd", 3)
@@ -170,24 +218,11 @@ def tile_generator_pa_t_kernel(tc, x, U, C, beta, gamma, bn_bias, out):
             elif g == 1:
                 transpose_x(2, "xt", 1)
 
-        half_rank = RANK // 2
-        regroup_u("scalar", 0, half_rank, RANK)
-        vector_part = small.tile([P, 2], F32)
-        nc.vector.bn_aggr(out=vector_part[:], in_=stats[:].rearrange("p s d -> p (s d)"))
-        nc.vector.scalar_tensor_tensor(
-            out=vector_part[:, 1:2],
-            in0=vector_part[:, 0:1],
-            scalar=vector_part[:, 0:1],
-            in1=vector_part[:, 1:2],
-            op0=ALU.mult,
-            op1=ALU.add,
-        )
-        affine_ps = psum.tile([P, 2, 2], F32, tag="even", bufs=2)
-        for k in range(2):
-            nc.tensor.matmul(
-                out=affine_ps[:, k, :], lhsT=ones_bf[:], rhs=affine_rows[k][:], start=True, stop=True
-            )
+        regroup_u("scalar", 0, RANK//2, RANK)
+        pixel_sum = small.tile([P, 1], F32)
+        nc.vector.tensor_copy(out=pixel_sum[:], in_=pixel_sums[:])
         diagonal = small.tile([P, P], F32)
+        gram_squares = small.tile([P, 1], F32)
         nc.vector.scalar_tensor_tensor(
             out=diagonal[:],
             in0=gram[:],
@@ -195,41 +230,50 @@ def tile_generator_pa_t_kernel(tc, x, U, C, beta, gamma, bn_bias, out):
             in1=ident_f32[:],
             op0=ALU.mult,
             op1=ALU.mult,
-            accum_out=squares[:, GROUPS : GROUPS + 1],
+            accum_out=gram_squares[:],
         )
-        sums = small.tile([P, 2], F32)
-        nc.vector.tensor_copy(out=sums[:, 0:1], in_=pixel_sums[:])
-        nc.vector.tensor_reduce(out=sums[:, 1:2], in_=squares[:], axis=AXIS.X, op=ALU.add)
-        moments_ps = psum.tile([P, 2], F32, tag="o", bufs=2)
-        nc.tensor.matmul(
-            out=moments_ps[:], lhsT=vector_share[:], rhs=vector_part[:], start=True, stop=False
+
+        def add_up(parts):
+            total = psum.tile([P, 1], F32, tag="even", bufs=2, name="total")
+            for k, (weight, column) in enumerate(parts):
+                nc.tensor.matmul(
+                    out=total[:], lhsT=weight[:], rhs=column, start=(k == 0), stop=(k == len(parts) - 1)
+                )
+            return total
+
+        mean = add_up([(vector_share, vector_part[:, 0:1]), (inv_count, pixel_sum[:])])
+        mean_of_squares = add_up(
+            [(vector_share, vector_part[:, 1:2]), (inv_count, early_squares[:])]
+            + [(inv_count, squares[:, s : s + 1]) for s in range(early, SCALAR_TOTAL)]
+            + [(inv_count, gram_squares[:])]
         )
-        nc.tensor.matmul(out=moments_ps[:], lhsT=inv_count[:], rhs=sums[:], start=False, stop=True)
-        regroup_u("vector", 0, 0, half_rank // 2)
-        affine = small.tile([P, 2, 2], F32)
-        nc.vector.tensor_copy(out=affine[:], in_=affine_ps[:])
-        minus = small.tile([P, 2], F32)
+        regroup_u("vector", 0, 0, RANK//4)
+        mean_squared = small.tile([P, 1], F32)
         nc.vector.tensor_scalar(
-            out=minus[:], in0=moments_ps[:], scalar1=-1.0, scalar2=None, op0=ALU.mult
+            out=mean_squared[:], in0=mean[:], scalar1=mean[:], scalar2=None, op0=ALU.mult
         )
-        minus_var = small.tile([P, 1], F32)
-        nc.vector.scalar_tensor_tensor(
-            out=minus_var[:],
-            in0=minus[:, 0:1],
-            scalar=minus[:, 0:1],
-            in1=minus[:, 1:2],
-            op0=ALU.mult,
-            op1=ALU.add,
+        squares_eps = small.tile([P, 1], F32)
+        nc.vector.tensor_scalar(
+            out=squares_eps[:], in0=mean_of_squares[:], scalar1=EPS, scalar2=None, op0=ALU.add
         )
         minus_product = small.tile([P, 1], F32)
-        nc.vector.tensor_tensor(
-            out=minus_product[:], in0=minus[:, 0:1], in1=affine[:, 0, 0:1], op=ALU.mult
+        nc.vector.scalar_tensor_tensor(
+            out=minus_product[:],
+            in0=mean[:],
+            scalar=-1.0,
+            in1=affine[:, 0, 0:1],
+            op0=ALU.mult,
+            op1=ALU.mult,
         )
         rstd = small.tile([P, 1], F32)
         nc.scalar.activation(
-            out=rstd[:], in_=minus_var[:], func=ACT.Abs_reciprocal_sqrt, scale=-1.0, bias=EPS
+            out=rstd[:],
+            in_=mean_squared[:],
+            func=ACT.Abs_reciprocal_sqrt,
+            scale=-1.0,
+            bias=squares_eps[:],
         )
-        regroup_u("vector", 0, half_rank // 2, half_rank)
+        regroup_u("vector", 0, RANK//4, RANK//2)
         gain = small.tile([P, 1], F32)
         nc.vector.tensor_tensor(out=gain[:], in0=rstd[:], in1=affine[:, 0, 0:1], op=ALU.mult)
         shift = small.tile([P, 1], F32)
@@ -392,6 +436,11 @@ def tile_generator_pa_t_kernel(tc, x, U, C, beta, gamma, bn_bias, out):
 
         for step in range(H_LAG):
             open_step(step)
+        def multiply_even(j):
+            for n in (0, 2):
+                multiply_u(j, n)
+                copy_t(j, n)
+
         normalise("vector", 0)
         normalise("vector", 1)
         quantise(0, 0, PAIR_ROWS)
@@ -402,16 +451,11 @@ def tile_generator_pa_t_kernel(tc, x, U, C, beta, gamma, bn_bias, out):
         quantise_u(2)
         regroup_u("vector", 3, 0, RANK)
         quantise_u(1)
+        multiply_even(0)
         quantise_u(3)
 
-        shared_blocks = (3, 7)
+        shared_blocks = ()
 
-        def multiply_even(j):
-            for n in (0, 2):
-                multiply_u(j, n)
-                copy_t(j, n)
-
-        multiply_even(0)
         for j in range(BLOCKS):
             pair, half = divmod(j, 2)
             if half == 0:
@@ -466,4 +510,4 @@ def tile_generator_pa_t_kernel(tc, x, U, C, beta, gamma, bn_bias, out):
                 quantise(PAIRS - 1 + H_LAG, PAIR_ROWS, 2 * PAIR_ROWS)
             if j + OUT_LAG - C_LAG + 1 < BLOCKS:
                 multiply_c(j + OUT_LAG - C_LAG + 1, *tail_bank(j))
-            add_beta(j, j % 2 == 1 and j < BLOCKS - 1)
+            add_beta(j, j == BLOCKS - 3)

@@ -53,7 +53,7 @@ def tile_generator_pa_t_kernel(tc, x, U, C, beta, gamma, bn_bias, out):
         name="stage", bufs=2
     ) as stage, tc.tile_pool(name="work", bufs=3) as work, tc.psum_pool(
         name="psum", bufs=1
-    ) as psum, tc.manual_schedule():
+    ) as psum:
         affine_rows = []
         for vector in (gamma, bn_bias):
             row = const.tile([P, 2], BF16, name="row%d" % len(affine_rows))

@@ -34,8 +34,8 @@ SCALAR_TOTAL = sum(SCALAR_BLOCKS)
 H_LAG = 3
 VALUE_BUFS = 6
 CODE_BUFS = 6
-C_LAG = 5
-OUT_LAG = 6
+C_LAG = 6
+OUT_LAG = 7
 
 TERM_ORDER = (0, 2, 1, 3)
 
@@ -183,7 +183,7 @@ def tile_generator_pa_t_kernel(tc, x, U, C, beta, gamma, bn_bias, out):
                 nc.vector.tensor_reduce(
                     out=early_squares[:], in_=squares[:, :early], axis=AXIS.X, op=ALU.add
                 )
-                affine_ps = psum.tile([P, 2, 2], F32, tag="odd", bufs=3)
+                affine_ps = psum.tile([P, 2, 2], F32, tag="bank", bufs=6)
                 for k in range(2):
                     nc.tensor.matmul(
                         out=affine_ps[:, k, :],
@@ -213,10 +213,10 @@ def tile_generator_pa_t_kernel(tc, x, U, C, beta, gamma, bn_bias, out):
                             stop=(last_group and jj == GROUP - 1 and c == PIXELS // P - 1),
                         )
             if g == 0:
-                transpose_x(0, "odd", 3)
-                transpose_x(1, "odd", 3)
+                transpose_x(0, "bank", 6)
+                transpose_x(1, "bank", 6)
             elif g == 1:
-                transpose_x(2, "xt", 1)
+                transpose_x(2, "bank", 6)
 
         regroup_u("scalar", 0, RANK//2, RANK)
         pixel_sum = small.tile([P, 1], F32)
@@ -234,7 +234,7 @@ def tile_generator_pa_t_kernel(tc, x, U, C, beta, gamma, bn_bias, out):
         )
 
         def add_up(parts):
-            total = psum.tile([P, 1], F32, tag="even", bufs=2, name="total")
+            total = psum.tile([P, 1], F32, tag="bank", bufs=6, name="total")
             for k, (weight, column) in enumerate(parts):
                 nc.tensor.matmul(
                     out=total[:], lhsT=weight[:], rhs=column, start=(k == 0), stop=(k == len(parts) - 1)
@@ -363,8 +363,8 @@ def tile_generator_pa_t_kernel(tc, x, U, C, beta, gamma, bn_bias, out):
             t_n = psum.tile(
                 [P, CHUNKS, P],
                 F32,
-                tag="odd" if n % 2 else "even",
-                bufs=3 if n % 2 else 2,
+                tag="bank",
+                bufs=6,
                 name="t",
             )
             for r in range(CHUNKS):
@@ -484,7 +484,7 @@ def tile_generator_pa_t_kernel(tc, x, U, C, beta, gamma, bn_bias, out):
                 for n in (1, 3):
                     multiply_u(j, n)
                 if pair + 3 < PAIRS:
-                    transpose_x(pair + 3, "xt", 1)
+                    transpose_x(pair + 3, "bank", 6)
                 if j in (2, 2 + 1):
                     transpose_c(j - 2)
                     copy_c(j - 2)
@@ -502,7 +502,7 @@ def tile_generator_pa_t_kernel(tc, x, U, C, beta, gamma, bn_bias, out):
                 multiply_h(nc.vector if j == BLOCKS - 1 else nc.gpsimd, j)
 
         def tail_bank(j):
-            return ("even", 2) if j % 2 else ("odd", 3)
+            return ("bank", 6)
 
         multiply_c(BLOCKS - C_LAG)
         for j in range(BLOCKS - OUT_LAG, BLOCKS):

import concourse.bass as bass
import concourse.mybir as mybir
import concourse.tile as tile
from concourse.masks import make_identity

F32 = mybir.dt.float32
BF16 = mybir.dt.bfloat16
U32 = mybir.dt.uint32
U8 = mybir.dt.uint8
FP8X4 = mybir.dt.float8_e4m3fn_x4
ACT = mybir.ActivationFunctionType
ALU = mybir.AluOpType
AXIS = mybir.AxisListType

P = 128
BATCH = 4096
PIXELS = 512
RANK = 512
DEGREE = 4
EPS = 1e-5
BLOCKS = BATCH // P
GROUP = 4
GROUPS = BLOCKS // GROUP
PAIRS = BLOCKS // 2
PAIR_ROWS = 2 * P
CHUNKS = RANK // P
COUNT = BATCH * PIXELS

VECTOR_BLOCKS = [2, 2, 2, 2, 2, 2, 1, 0]
SCALAR_BLOCKS = [1, 1, 1, 1, 1, 1, 1, 2]
VECTOR_TOTAL = sum(VECTOR_BLOCKS)
SCALAR_TOTAL = sum(SCALAR_BLOCKS)

H_LAG = 3
VALUE_BUFS = 6
CODE_BUFS = 6
C_LAG = 6
OUT_LAG = 7

TERM_ORDER = (0, 2, 1, 3)

FLOPS = 2 * BATCH * PIXELS * RANK * (DEGREE + 1)


def tile_generator_pa_t_kernel(tc, x, U, C, beta, gamma, bn_bias, out):
    nc = tc.nc
    x_rows = x.rearrange("(p j) o h w -> p j (o h w)", j=BLOCKS)
    out_rows = out.rearrange("(p j) o h w -> p j (o h w)", j=BLOCKS)

    with tc.tile_pool(name="const", bufs=1) as const, tc.tile_pool(
        name="keep", bufs=1
    ) as keep, tc.tile_pool(name="small", bufs=1) as small, tc.tile_pool(
        name="stage", bufs=2
    ) as stage, tc.tile_pool(name="work", bufs=3) as work, tc.psum_pool(
        name="psum", bufs=1
    ) as psum:
        affine_rows = []
        for vector in (gamma, bn_bias):
            row = const.tile([P, 2], BF16, name="row%d" % len(affine_rows))
            nc.vector.memset(row[:], 0.0)
            nc.scalar.dma_start(out=row[0:1, 0:1], in_=vector.rearrange("(a b) -> a b", a=1))
            affine_rows.append(row)
        x_sb = []
        for g in range(GROUPS):
            x_g = keep.tile([P, GROUP, PIXELS], BF16, name="x%d" % g)
            nc.sync.dma_start(out=x_g[:], in_=x_rows[:, g * GROUP : (g + 1) * GROUP, :])
            x_sb.append(x_g)
        u_raw = {}
        for n in TERM_ORDER:
            u_n = keep.tile([P, 4, RANK], BF16, name="u_raw%d" % n)
            nc.sync.dma_start(
                out=u_n[:].rearrange("w (u e) c -> w u (e c)", u=2),
                in_=U[n].rearrange("(u w e) c -> w u (e c)", u=2, e=2),
            )
            u_raw[n] = u_n
        c_raw = keep.tile([P, CHUNKS, RANK], BF16)
        nc.sync.dma_start(out=c_raw[:], in_=C.rearrange("(q p) r -> p q r", p=P))
        beta_bc = const.tile([P, PIXELS], BF16)
        nc.sync.dma_start(out=beta_bc[:], in_=beta.partition_broadcast(P))

        one_t = const.tile([P, 1], F32)
        nc.vector.memset(one_t[:], 1.0)
        warm = const.tile([P, 1], F32)
        nc.scalar.activation(out=warm[:], in_=one_t[:], func=ACT.Abs_reciprocal_sqrt)
        ones_bf = const.tile([P, P], BF16)
        nc.vector.memset(ones_bf[:], 1.0)
        vector_share = const.tile([P, P], F32)
        nc.vector.memset(vector_share[:], VECTOR_TOTAL * PIXELS / COUNT)
        inv_count = const.tile([P, P], F32)
        nc.vector.memset(inv_count[:], 1.0 / COUNT)
        ident_f32 = const.tile([P, P], F32)
        make_identity(nc, ident_f32[:])
        ident_bf = const.tile([P, P], BF16)
        make_identity(nc, ident_bf[:])

        u_codes = keep.tile([P, DEGREE, RANK], U32, align_bytes=64)
        u_scales = keep.tile([P, DEGREE, RANK], U8, align_bytes=64)
        u_values = {}

        for n in TERM_ORDER:
            u_values[n] = keep.tile([P, RANK, 4], BF16, name="u_grp%d" % n, align_bytes=64)

        def regroup_u(engine, n, lo, hi):
            dst = u_values[n][:, lo:hi, :].rearrange("p (c i) t -> p c t i", i=4)
            src = u_raw[n][:, :, lo:hi].rearrange("p t (c i) -> p c t i", i=4)
            if engine == "scalar":
                nc.scalar.copy(out=dst, in_=src)
            else:
                nc.vector.tensor_copy(out=dst, in_=src)

        def spread_u(n):
            for ranks in (slice(0, RANK // 2), slice(RANK // 2, RANK)):
                grouped = psum.tile(
                    [P, RANK // 2, 4], BF16, tag="o" if ranks.start else "even", bufs=2, name="grouped"
                )
                for u in range(2):
                    nc.tensor.matmul(
                        out=grouped[:, :, 2 * u : 2 * u + 2],
                        lhsT=ident_bf[:],
                        rhs=u_raw[n][:, 2 * u : 2 * u + 2, ranks].rearrange("w e c -> w c e"),
                        start=True,
                        stop=True,
                    )
                nc.scalar.copy(out=u_values[n][:, ranks, :], in_=grouped[:])

        def quantise_u(n):
            nc.vector.quantize_mx(
                out=u_codes[:, n, :].bitcast(FP8X4),
                scales=u_scales[:, n, :],
                in_=u_values[n][:].rearrange("p c t -> p (c t)"),
            )

        xt_banks = {}

        def transpose_x(pair, tag, bufs):
            xt = psum.tile([P, 2, PAIR_ROWS], F32, tag=tag, bufs=bufs, name="xt")
            for side in range(2):
                g, jj = divmod(2 * pair + side, GROUP)
                words = x_sb[g][:, jj, :].bitcast(F32)
                for u in range(2):
                    nc.tensor.transpose(
                        xt[:, u, side * P : (side + 1) * P],
                        words[:, u * P : (u + 1) * P],
                        ident_f32[:],
                    )
            xt_banks[pair] = xt

        stats = small.tile([P, VECTOR_TOTAL, 6], F32)
        squares = small.tile([P, SCALAR_TOTAL], F32)
        gram = psum.tile([P, P], F32, tag="o", bufs=2)
        pixel_sums = psum.tile([P, 1], F32, tag="o", bufs=2)
        v_seen = 0
        s_seen = 0
        for g in range(GROUPS):
            last_group = g == GROUPS - 1
            v_end = VECTOR_BLOCKS[g]
            s_end = v_end + SCALAR_BLOCKS[g]
            for jj in range(v_end):
                nc.vector.bn_stats(out=stats[:, v_seen, :], in_=x_sb[g][:, jj, :])
                v_seen += 1
            for jj in range(v_end, s_end):
                unread = stage.tile([P, PIXELS], BF16, tag="unread")
                nc.scalar.activation(
                    out=unread[:],
                    in_=x_sb[g][:, jj, :],
                    func=ACT.Square,
                    accum_out=squares[:, s_seen : s_seen + 1],
                )
                s_seen += 1
            if last_group:
                vector_part = small.tile([P, 2], F32)
                nc.vector.bn_aggr(out=vector_part[:], in_=stats[:].rearrange("p s d -> p (s d)"))
                nc.vector.scalar_tensor_tensor(
                    out=vector_part[:, 1:2],
                    in0=vector_part[:, 0:1],
                    scalar=vector_part[:, 0:1],
                    in1=vector_part[:, 1:2],
                    op0=ALU.mult,
                    op1=ALU.add,
                )
                early = SCALAR_TOTAL - SCALAR_BLOCKS[g]
                early_squares = small.tile([P, 1], F32)
                nc.vector.tensor_reduce(
                    out=early_squares[:], in_=squares[:, :early], axis=AXIS.X, op=ALU.add
                )
                affine_ps = psum.tile([P, 2, 2], F32, tag="bank", bufs=6)
                for k in range(2):
                    nc.tensor.matmul(
                        out=affine_ps[:, k, :],
                        lhsT=ones_bf[:],
                        rhs=affine_rows[k][:],
                        start=True,
                        stop=True,
                    )
                affine = small.tile([P, 2, 2], F32)
                nc.vector.tensor_copy(out=affine[:], in_=affine_ps[:])
            for jj in range(v_end, GROUP):
                for c in range(PIXELS // P):
                    cols = x_sb[g][:, jj, c * P : (c + 1) * P]
                    nc.tensor.matmul(
                        out=pixel_sums[:],
                        lhsT=cols,
                        rhs=ones_bf[:, 0:1],
                        start=(g == 0 and jj == v_end and c == 0),
                        stop=(last_group and jj == GROUP - 1 and c == PIXELS // P - 1),
                    )
                    if jj >= s_end:
                        nc.tensor.matmul(
                            out=gram[:],
                            lhsT=cols,
                            rhs=cols,
                            start=(g == 0 and jj == s_end and c == 0),
                            stop=(last_group and jj == GROUP - 1 and c == PIXELS // P - 1),
                        )
            if g == 0:
                transpose_x(0, "bank", 6)
                transpose_x(1, "bank", 6)
            elif g == 1:
                transpose_x(2, "bank", 6)

        regroup_u("scalar", 0, RANK//2, RANK)
        pixel_sum = small.tile([P, 1], F32)
        nc.vector.tensor_copy(out=pixel_sum[:], in_=pixel_sums[:])
        diagonal = small.tile([P, P], F32)
        gram_squares = small.tile([P, 1], F32)
        nc.vector.scalar_tensor_tensor(
            out=diagonal[:],
            in0=gram[:],
            scalar=1.0,
            in1=ident_f32[:],
            op0=ALU.mult,
            op1=ALU.mult,
            accum_out=gram_squares[:],
        )

        def add_up(parts):
            total = psum.tile([P, 1], F32, tag="bank", bufs=6, name="total")
            for k, (weight, column) in enumerate(parts):
                nc.tensor.matmul(
                    out=total[:], lhsT=weight[:], rhs=column, start=(k == 0), stop=(k == len(parts) - 1)
                )
            return total

        mean = add_up([(vector_share, vector_part[:, 0:1]), (inv_count, pixel_sum[:])])
        mean_of_squares = add_up(
            [(vector_share, vector_part[:, 1:2]), (inv_count, early_squares[:])]
            + [(inv_count, squares[:, s : s + 1]) for s in range(early, SCALAR_TOTAL)]
            + [(inv_count, gram_squares[:])]
        )
        regroup_u("vector", 0, 0, RANK//4)
        mean_squared = small.tile([P, 1], F32)
        nc.vector.tensor_scalar(
            out=mean_squared[:], in0=mean[:], scalar1=mean[:], scalar2=None, op0=ALU.mult
        )
        squares_eps = small.tile([P, 1], F32)
        nc.vector.tensor_scalar(
            out=squares_eps[:], in0=mean_of_squares[:], scalar1=EPS, scalar2=None, op0=ALU.add
        )
        minus_product = small.tile([P, 1], F32)
        nc.vector.scalar_tensor_tensor(
            out=minus_product[:],
            in0=mean[:],
            scalar=-1.0,
            in1=affine[:, 0, 0:1],
            op0=ALU.mult,
            op1=ALU.mult,
        )
        rstd = small.tile([P, 1], F32)
        nc.scalar.activation(
            out=rstd[:],
            in_=mean_squared[:],
            func=ACT.Abs_reciprocal_sqrt,
            scale=-1.0,
            bias=squares_eps[:],
        )
        regroup_u("vector", 0, RANK//4, RANK//2)
        gain = small.tile([P, 1], F32)
        nc.vector.tensor_tensor(out=gain[:], in0=rstd[:], in1=affine[:, 0, 0:1], op=ALU.mult)
        shift = small.tile([P, 1], F32)
        nc.vector.scalar_tensor_tensor(
            out=shift[:],
            in0=rstd[:],
            scalar=minus_product[:],
            in1=affine[:, 1, 0:1],
            op0=ALU.mult,
            op1=ALU.add,
        )

        values = {}
        codes = {}
        z_at = {}
        h_at = {}

        def open_step(step):
            values[step] = work.tile(
                [P, 2, PAIR_ROWS, CHUNKS], BF16, tag="values", name="values", bufs=VALUE_BUFS, align_bytes=64
            )
            codes[step] = (
                work.tile([P, 2, PAIR_ROWS], U32, tag="codes", name="codes", bufs=CODE_BUFS, align_bytes=64),
                work.tile([P, 2, PAIR_ROWS], U8, tag="scales", name="scales", bufs=CODE_BUFS, align_bytes=64),
            )

        def normalise(engine, pair):
            dst = values[pair][:, 0, :, :].rearrange("w c (u e) -> w c u e", e=2)
            src = xt_banks[pair][:].bitcast(BF16).rearrange("w u (c e) -> w c u e", e=2)
            if engine == "scalar":
                nc.scalar.activation(
                    out=dst, in_=src, func=ACT.Identity, scale=gain[:], bias=shift[:]
                )
            else:
                nc.vector.tensor_scalar(
                    out=dst, in0=src, scalar1=gain[:], scalar2=shift[:], op0=ALU.mult, op1=ALU.add
                )

        def quantise(step, lo, hi):
            step_codes, step_scales = codes[step]
            nc.vector.quantize_mx(
                out=step_codes[:].rearrange("p k b -> p (k b)")[:, lo:hi].bitcast(FP8X4),
                scales=step_scales[:].rearrange("p k b -> p (k b)")[:, lo:hi],
                in_=values[step][:].rearrange("p k b r -> p (k b r)")[:, CHUNKS * lo : CHUNKS * hi],
            )

        c_codes = keep.tile([P, PIXELS], U32, align_bytes=64)
        c_scales = keep.tile([P, PIXELS], U8, align_bytes=64)
        c_grp = keep.tile([P, PIXELS, CHUNKS], BF16, align_bytes=64)
        ct_banks = {}

        def transpose_c(half):
            ct = psum.tile([P, CHUNKS, 2 * P], BF16, tag="o", bufs=2)
            for qq in range(2):
                for r in range(CHUNKS):
                    nc.tensor.transpose(
                        ct[:, r, qq * P : (qq + 1) * P],
                        c_raw[:, 2 * half + qq, r * P : (r + 1) * P],
                        ident_bf[:],
                    )
            ct_banks[half] = ct

        def copy_c(half):
            nc.scalar.copy(
                out=c_grp[:, 2 * half * P : 2 * (half + 1) * P, :],
                in_=ct_banks[half][:].rearrange("p r x -> p x r"),
            )

        def quantise_c():
            nc.vector.quantize_mx(
                out=c_codes[:].bitcast(FP8X4),
                scales=c_scales[:],
                in_=c_grp[:].rearrange("p x r -> p (x r)"),
            )

        t_banks = {}
        t_copies = {}
        factors = {}
        o_banks = {}

        def rows_of(j):
            return slice((j % 2) * P, (j % 2 + 1) * P)

        def multiply_u(j, n):
            z_codes, z_scales = codes[j // 2]
            rows = rows_of(j)
            t_n = psum.tile(
                [P, CHUNKS, P],
                F32,
                tag="bank",
                bufs=6,
                name="t",
            )
            for r in range(CHUNKS):
                ranks = slice(r * P, (r + 1) * P)
                nc.tensor.matmul_mx(
                    out=t_n[:, r, :],
                    lhsT=u_codes[:, n, ranks].bitcast(FP8X4),
                    lhsT_scale=u_scales[:, n, ranks],
                    rhs=z_codes[:, 0, rows].bitcast(FP8X4),
                    rhs_scale=z_scales[:, 0, rows],
                    start=True,
                    stop=True,
                )
            t_banks[j, n] = t_n[:].rearrange("p r b -> p b r")

        def copy_t(j, n):
            t_sb = work.tile([P, P, CHUNKS], F32, tag="t%d_sb" % n, name="t_sb")
            if n == 0:
                nc.scalar.copy(out=t_sb[:], in_=t_banks[j, n])
            else:
                nc.scalar.activation(out=t_sb[:], in_=t_banks[j, n], func=ACT.Copy, bias=1.0)
            t_copies[j, n] = t_sb

        def multiply_terms(j, n):
            factor = work.tile([P, P, CHUNKS], F32, tag="factor%d" % n, name="factor")
            nc.vector.scalar_tensor_tensor(
                out=factor[:],
                in0=t_banks[j, n + 1],
                scalar=1.0,
                in1=t_copies[j, n][:],
                op0=ALU.add,
                op1=ALU.mult,
            )
            factors[j, n] = factor

        def multiply_h(engine, j):
            engine.tensor_tensor(
                out=values[j // 2 + H_LAG][:, 1, rows_of(j), :],
                in0=factors[j, 0][:],
                in1=factors[j, 2][:],
                op=ALU.mult,
            )

        def multiply_c(j, tag="o", bufs=2):
            h_codes, h_scales = codes[j // 2 + H_LAG]
            rows = rows_of(j)
            o = psum.tile([P, PIXELS], F32, tag=tag, bufs=bufs, name="o")
            nc.tensor.matmul_mx(
                out=o[:],
                lhsT=h_codes[:, 1, rows].bitcast(FP8X4),
                lhsT_scale=h_scales[:, 1, rows],
                rhs=c_codes[:].bitcast(FP8X4),
                rhs_scale=c_scales[:],
                start=True,
                stop=True,
            )
            o_banks[j] = o

        def add_beta(j, shared):
            out_sb = work.tile([P, PIXELS], F32, tag="out_sb", bufs=8)
            o = o_banks[j]
            if shared:
                o_sb = work.tile([P, PIXELS], F32, tag="o_sb")
                nc.scalar.copy(out=o_sb[:], in_=o[:])
                nc.gpsimd.tensor_tensor(out=out_sb[:], in0=o_sb[:], in1=beta_bc[:], op=ALU.add)
            else:
                nc.vector.tensor_tensor(out=out_sb[:], in0=o[:], in1=beta_bc[:], op=ALU.add)
            nc.sync.dma_start(out=out_rows[:, j, :], in_=out_sb[:])

        for step in range(H_LAG):
            open_step(step)
        def multiply_even(j):
            for n in (0, 2):
                multiply_u(j, n)
                copy_t(j, n)

        normalise("vector", 0)
        normalise("vector", 1)
        quantise(0, 0, PAIR_ROWS)
        regroup_u("scalar", 2, 0, RANK)
        regroup_u("scalar", 1, 0, RANK)
        quantise_u(0)
        quantise(1, 0, PAIR_ROWS)
        quantise_u(2)
        regroup_u("vector", 3, 0, RANK)
        quantise_u(1)
        multiply_even(0)
        quantise_u(3)

        shared_blocks = ()

        for j in range(BLOCKS):
            pair, half = divmod(j, 2)
            if half == 0:
                open_step(pair + H_LAG)
                if j + 1 < BLOCKS:
                    multiply_even(j + 1)
                for n in (1, 3):
                    multiply_u(j, n)
                if pair + 2 < PAIRS:
                    normalise("vector" if pair < 2 else "scalar", pair + 2)
                if j in (2, 2 + 1):
                    transpose_c(j - 2)
                    copy_c(j - 2)
                if j >= OUT_LAG:
                    add_beta(j - OUT_LAG, (j - OUT_LAG) % 8 in shared_blocks)
                if j >= C_LAG:
                    multiply_c(j - C_LAG)
                multiply_terms(j, 0)
                multiply_terms(j, 2)
                if j == 4:
                    quantise_c()
                multiply_h(nc.vector if j == BLOCKS - 1 else nc.gpsimd, j)
            else:
                if j + 1 < BLOCKS:
                    multiply_even(j + 1)
                for n in (1, 3):
                    multiply_u(j, n)
                if pair + 3 < PAIRS:
                    transpose_x(pair + 3, "bank", 6)
                if j in (2, 2 + 1):
                    transpose_c(j - 2)
                    copy_c(j - 2)
                if j >= OUT_LAG:
                    add_beta(j - OUT_LAG, (j - OUT_LAG) % 8 in shared_blocks)
                if j >= C_LAG:
                    multiply_c(j - C_LAG)
                multiply_terms(j, 0)
                multiply_terms(j, 2)
                first = 0 if pair + 2 < PAIRS else PAIR_ROWS
                last = 2 * PAIR_ROWS if pair + 2 >= H_LAG else PAIR_ROWS
                quantise(pair + 2, first, last)
                if j == 4:
                    quantise_c()
                multiply_h(nc.vector if j == BLOCKS - 1 else nc.gpsimd, j)

        def tail_bank(j):
            return ("bank", 6)

        multiply_c(BLOCKS - C_LAG)
        for j in range(BLOCKS - OUT_LAG, BLOCKS):
            if j == BLOCKS - OUT_LAG + 1:
                quantise(PAIRS - 1 + H_LAG, PAIR_ROWS, 2 * PAIR_ROWS)
            if j + OUT_LAG - C_LAG + 1 < BLOCKS:
                multiply_c(j + OUT_LAG - C_LAG + 1, *tail_bank(j))
            add_beta(j, j == BLOCKS - 3)
